import numpy as np
import ml_dtypes


def mxq(x, axis, fmt="e4m3"):
    dtype, down = {"e4m3": (ml_dtypes.float8_e4m3fn, 7), "e5m2": (ml_dtypes.float8_e5m2, 14)}[fmt]
    v = np.moveaxis(np.asarray(x, np.float32).astype(ml_dtypes.bfloat16).astype(np.float64), axis, -1)
    blocks = v.reshape(v.shape[:-1] + (-1, 32))
    amax = np.abs(blocks).max(-1, keepdims=True)
    byte = np.maximum(np.where(amax > 0, np.frexp(amax)[1] - 1 + 127, 0) - down, 1)
    scale = np.exp2(byte - 127.0)
    codes = (blocks / scale).astype(np.float32).astype(dtype).astype(np.float64)
    return np.moveaxis((codes * scale).reshape(v.shape), -1, axis)


WIDE = False


def mx_kscale(k):
    if not WIDE:
        return np.ones(k)
    levels = np.array([10, -10, 5, -5, 0])
    if k % 512:
        return np.exp2(np.random.permutation(np.resize(levels, k // 32))).repeat(32)
    a = np.empty((k // 512, 16))
    for p in range(k // 512):
        a[p, :8] = np.random.permutation(np.resize(levels, 8))
        for g in range(8):
            far = levels[np.abs(levels - a[p, g]) >= 10]
            a[p, g + 8] = far[np.random.randint(len(far))]
    return np.exp2(a.ravel()).repeat(32)


BF16 = ml_dtypes.bfloat16


def bf(x):
    return np.asarray(x, np.float32).astype(BF16)


def f64(x):
    return np.asarray(x).astype(np.float64)


E2M1 = np.array([0.0, 0.5, 1.0, 1.5, 2.0, 3.0, 4.0, 6.0, -0.0, -0.5, -1.0, -1.5, -2.0, -3.0, -4.0, -6.0])


def pack_weight(w, fmt):
    k, n = w.shape
    w = f64(bf(w)).reshape(k // 32, 32, n)
    amax = np.abs(w).max(1)
    if fmt == "e4m3":
        byte = np.frexp(amax)[1] - 1 + 127 - 7
    else:
        mant, ex = np.frexp(amax / 6.0)
        byte = np.where(mant > 0.5, ex, ex - 1) + 127
    byte = np.clip(np.where(amax > 0, byte, 1), 1, 254)
    scaled = (w * np.exp2(127.0 - byte)[:, None, :]).reshape(k, n).astype(np.float32)
    by_word = np.ascontiguousarray(scaled.reshape(k // 512, 128, 4, n).transpose(0, 1, 3, 2))
    if fmt == "e4m3":
        words = by_word.astype(ml_dtypes.float8_e4m3fn).view(np.uint8)
    else:
        c = by_word.astype(ml_dtypes.float4_e2m1fn).view(np.uint8) & 0xF
        words = c[..., 0::2] | (c[..., 1::2] << 4)
    return np.ascontiguousarray(words), np.ascontiguousarray(byte.astype(np.uint8).reshape(k // 512, 16, n))


def unpack_weight(words, scales, fmt):
    g, p, n, _ = words.shape
    if fmt == "e4m3":
        vals = np.ascontiguousarray(words).view(ml_dtypes.float8_e4m3fn).astype(np.float64)
    else:
        nib = np.empty((g, p, n, 4), np.uint8)
        nib[..., 0::2] = words & 0xF
        nib[..., 1::2] = words >> 4
        vals = E2M1[nib]
    vals = vals * np.repeat(np.exp2(scales.astype(np.float64) - 127.0), 8, axis=1)[..., None]
    return vals.transpose(0, 1, 3, 2).reshape(g * 512, n)


B, S, D, H, DN, DR, DV, RQ, RKV = 2, 256, 2048, 16, 64, 128, 128, 1536, 512
THETA = 10000.0
EPS = 1e-6


def rmsnorm(v, w):
    return v * (1.0 / np.sqrt(np.mean(v * v, axis=-1, keepdims=True) + EPS)) * w


def rotate_half(v):
    v1 = v[..., ::2]
    v2 = v[..., 1::2]
    return np.stack((-v2, v1), axis=-1).reshape(v.shape)


def rope_cache():
    inv_freq = 1.0 / THETA ** (np.arange(0, DR, 2) / DR)
    freqs = np.outer(np.arange(S), inv_freq)
    emb = np.concatenate((freqs, freqs), -1)
    return np.cos(emb), np.sin(emb)


def apply_rope(v, cos, sin):
    return v * cos[None, None] + rotate_half(v) * sin[None, None]


def draw0():
    s, t = mx_kscale(D), mx_kscale(RQ)
    x = bf(np.random.standard_normal((B, S, D)) * s)
    Wqa_words, Wqa_scales = pack_weight(np.random.standard_normal((D, RQ)) / np.sqrt(D) / s[:, None], "e4m3")
    q_a_norm_w = bf((1.0 + 0.1 * np.random.standard_normal(RQ)) * t)
    Wqb_words, Wqb_scales = pack_weight(np.random.standard_normal((RQ, H * (DN + DR))) / np.sqrt(RQ) / t[:, None], "e4m3")
    return {"x": x,
            "Wqa_words": Wqa_words, "Wqa_scales": Wqa_scales,
            "q_a_norm_w": q_a_norm_w,
            "Wqb_words": Wqb_words, "Wqb_scales": Wqb_scales}


def core(x, Wqa_words, Wqa_scales, q_a_norm_w, Wqb_words, Wqb_scales):
    c = mxq(f64(x), 2, "e4m3") @ unpack_weight(Wqa_words, Wqa_scales, "e4m3")
    h = rmsnorm(c, f64(q_a_norm_w))
    q = mxq(h, 2, "e4m3") @ unpack_weight(Wqb_words, Wqb_scales, "e4m3")
    q = q.reshape(B, S, H, DN + DR).transpose(0, 2, 1, 3)
    q_nope, q_rope = q[..., :DN], q[..., DN:]
    cos, sin = rope_cache()
    q_rope = apply_rope(q_rope, cos, sin)
    return np.concatenate([q_nope, q_rope], -1)


def e4m3fn_bytes(y):
    return np.clip(np.asarray(y, np.float64), -448.0, 448.0).astype(np.float32).astype(ml_dtypes.float8_e4m3fn).view(np.uint8)


def e4m3fn_values(b):
    return np.asarray(b, np.uint8).view(ml_dtypes.float8_e4m3fn).astype(np.float64)


def setup_inputs():
    d = draw0()
    x0 = np.asarray(d['x']).astype(np.float64)
    s = (np.max(np.abs(x0), axis=(0, 1), keepdims=True) / 448.0).astype(np.float32)
    out = {}
    for k, v in d.items():
        if k == 'x':
            out['x_bytes'] = e4m3fn_bytes(x0 / s.astype(np.float64))
            out['x_scale'] = s
        else:
            out[k] = v
    return out


def reference(x_bytes, x_scale, Wqa_words, Wqa_scales, q_a_norm_w, Wqb_words, Wqb_scales):
    return core(e4m3fn_values(x_bytes) * x_scale.astype(np.float64), Wqa_words, Wqa_scales, q_a_norm_w, Wqb_words, Wqb_scales)

@@ -1,0 +1,569 @@
+import math
+from contextlib import ExitStack
+
+import concourse.mybir as mybir
+from concourse.masks import make_identity
+
+B, S, D, H, DN, DR, RQ = 2, 256, 2048, 16, 64, 128, 1536
+DH = DN + DR
+NQ = H * DH
+THETA = 10000.0
+EPS = 1e-6
+P = 128
+FLOPS = 2 * B * S * D * RQ + 2 * B * S * RQ * NQ
+
+F32 = mybir.dt.float32
+BF16 = mybir.dt.bfloat16
+I32 = mybir.dt.int32
+U32 = mybir.dt.uint32
+U8 = mybir.dt.uint8
+FP8 = mybir.dt.float8_e4m3fn
+FP8X4 = mybir.dt.float8_e4m3fn_x4
+ADD = mybir.AluOpType.add
+SUB = mybir.AluOpType.subtract
+MUL = mybir.AluOpType.mult
+ACT = mybir.ActivationFunctionType
+AX = mybir.AxisListType
+
+GA = D // 512
+GB = RQ // 512
+NB = NQ // 512
+
+
+def tile_multiheadlatentattention_pa_w8_kernel(
+    tc, x_bytes, x_scale, Wqa_words, Wqa_scales, q_a_norm_w, Wqb_words, Wqb_scales, out
+):
+    nc = tc.nc
+    with ExitStack() as ctx:
+        keep = ctx.enter_context(tc.tile_pool(name="keep", bufs=1))
+        work = ctx.enter_context(tc.tile_pool(name="work", bufs=4))
+        psum = ctx.enter_context(tc.psum_pool(name="psum", bufs=1))
+        ctx.enter_context(tc.manual_schedule())
+
+        x8 = [keep.tile([P, D], U8, name="x8_%d" % (i,)) for i in range(4)]
+        xb = [keep.tile([P, D], BF16, name="xb_%d" % (i,), align_bytes=64) for i in range(4)]
+        xg = [keep.tile([P, D], BF16, name="xg_%d" % (i,), align_bytes=64) for i in range(4)]
+        xq = [keep.tile([P, GA * P], U32, name="xq_%d" % (i,), align_bytes=64) for i in range(4)]
+        xqs = [keep.tile([P, GA * P], U8, name="xqs_%d" % (i,), align_bytes=64) for i in range(4)]
+        hb = [keep.tile([P, RQ], BF16, name="hb_%d" % (i,), align_bytes=64) for i in range(4)]
+        hg = [keep.tile([P, RQ], BF16, name="hg_%d" % (i,), align_bytes=64) for i in range(4)]
+        hq = [keep.tile([P, GB * P], U32, name="hq_%d" % (i,), align_bytes=64) for i in range(4)]
+        hqs = [keep.tile([P, GB * P], U8, name="hqs_%d" % (i,), align_bytes=64) for i in range(4)]
+        ssq = [keep.tile([P, 8], F32, name="ssq_%d" % (i,)) for i in range(4)]
+        rms = [keep.tile([P, 8], F32, name="rms_%d" % (i,)) for i in range(4)]
+        wa = [keep.tile([P, GA, 512], U32, name="wa_%d" % (i,), align_bytes=64) for i in range(GB)]
+        wb = [keep.tile([P, GB, 512], U32, name="wb_%d" % (i,), align_bytes=64) for i in range(NB)]
+        was = keep.tile([P, RQ], U8, name="was", align_bytes=64)
+        wbs = keep.tile([P, NQ], U8, name="wbs", align_bytes=64)
+        xs = keep.tile([P, GA, 4], F32, name="xs")
+        gbc = keep.tile([P, RQ], BF16, name="gbc", align_bytes=64)
+        ones = keep.tile([P, P], BF16, name="ones", align_bytes=64)
+        ident = keep.tile([P, P], F32, name="ident", align_bytes=64)
+        pos = keep.tile([P, 2], I32, name="pos")
+        turns = keep.tile([P, 2, 64], F32, name="turns")
+        kint = keep.tile([P, 2, 2, 64], I32, name="kint")
+        frac = keep.tile([P, 2, 2, 64], F32, name="frac")
+        tab = keep.tile([P, 2, 2, P], F32, name="tab")
+        warm = keep.tile([P, 1], F32, name="warm")
+        osb = [keep.tile([P, H, 2, DH], F32, name="osb_%d" % (i,)) for i in range(2)]
+
+        def bank(i, shape, dtype, name):
+            return psum.tile(shape, dtype, name=name, tag="bank%d" % (i,), bufs=1)
+
+        nc.gpsimd.iota(pos[:], pattern=[[1, 2]], base=0, channel_multiplier=2)
+        make_identity(nc, ident[:])
+        nc.gpsimd.memset(wbs[:].bitcast(I32), 0)
+        nc.vector.memset(was[:].bitcast(I32), 0)
+        nc.vector.memset(ones[:], 1.0)
+
+        def load_x(i):
+            b, par = divmod(i, 2)
+            nc.sync.dma_start(
+                out=x8[i][:], in_=x_bytes[b].rearrange("(p two) k -> p two k", two=2)[:, par, :]
+            )
+
+        def load_scales(tile, dram, groups):
+            for q in range(4):
+                nc.sync.dma_start(
+                    out=tile[32 * q : 32 * q + 4 * groups, :].bitcast(I32),
+                    in_=dram[:, 4 * q : 4 * q + 4, :].bitcast(I32),
+                )
+
+        def load_w(tile, dram, n):
+            nc.sync.dma_start(
+                out=tile[:].bitcast(I32),
+                in_=dram.rearrange("g p n t -> p g (n t)")[:, :, 2048 * n : 2048 * (n + 1)].bitcast(I32),
+            )
+
+        nc.scalar.dma_start(out=xs[:], in_=x_scale.rearrange("a b (g p t) -> p (a b g) t", p=P, t=4))
+        load_x(0)
+        load_scales(was, Wqa_scales, GA)
+        load_x(1)
+        load_w(wa[0], Wqa_words, 0)
+        load_w(wa[1], Wqa_words, 1)
+        load_w(wa[2], Wqa_words, 2)
+        load_x(2)
+        load_x(3)
+        nc.sync.dma_start(out=gbc[:], in_=q_a_norm_w.partition_broadcast(P))
+        load_scales(wbs, Wqb_scales, GB)
+        for n in range(NB):
+            load_w(wb[n], Wqb_words, n)
+
+        nc.vector.tensor_scalar(out=turns[:, :, 0:1], in0=pos[:].unsqueeze(2), scalar1=1.0 / (2.0 * math.pi), scalar2=None, op0=MUL)
+        for j in range(6):
+            m = 1 << j
+            nc.vector.tensor_scalar(out=turns[:, :, m : 2 * m], in0=turns[:, :, 0:m], scalar1=THETA ** (-m / 64.0), scalar2=None, op0=MUL)
+        nc.vector.tensor_scalar(out=kint[:, 0], in0=turns[:], scalar1=0.25, scalar2=None, op0=ADD)
+        nc.vector.tensor_scalar(out=kint[:, 1], in0=turns[:], scalar1=0.0, scalar2=None, op0=ADD)
+        nc.vector.scalar_tensor_tensor(out=frac[:, 0], in0=turns[:], scalar=0.25, in1=kint[:, 0], op0=ADD, op1=SUB)
+        nc.vector.tensor_tensor(out=frac[:, 1], in0=turns[:], in1=kint[:, 1], op=SUB)
+        two_pi = 2.0 * math.pi
+        for half in range(2):
+            c0 = 64 * half
+            nc.scalar.activation(out=tab[:, :, 0, c0 : c0 + 64], in_=frac[:, 0], func=ACT.Sin, scale=two_pi)
+            nc.scalar.activation(out=tab[:, :, 1, c0 : c0 + 64 : 2], in_=frac[:, 1, :, 1::2], func=ACT.Sin, scale=two_pi)
+            nc.scalar.activation(out=tab[:, :, 1, c0 + 1 : c0 + 64 : 2], in_=frac[:, 1, :, 0::2], func=ACT.Sin, scale=-two_pi)
+
+        def cast_s(i, lo, hi):
+            nc.scalar.copy(out=xb[i][:, lo:hi], in_=x8[i][:, lo:hi].bitcast(FP8))
+
+        def cast_g(i, lo, hi):
+            nc.gpsimd.tensor_copy(out=xb[i][:, lo:hi], in_=x8[i][:, lo:hi].bitcast(FP8))
+
+        def cast_v(i, lo, hi):
+            nc.vector.tensor_copy(out=xb[i][:, lo:hi], in_=x8[i][:, lo:hi].bitcast(FP8))
+
+        trx = {}
+
+        def turn_x(i, half, b):
+            pt = bank(b, [P, 2, 2, P], F32, "trx%d_%d" % (i, half))
+            trx[i, half] = pt
+            words = xb[i][:].bitcast(F32)
+            for g in (2 * half, 2 * half + 1):
+                for u in range(2):
+                    nc.tensor.transpose(pt[:, g - 2 * half, u, :], words[:, 256 * g + u : 256 * (g + 1) : 2], ident[:])
+
+        def scale_x(i, g):
+            pt = trx[i, g // 2]
+            src = pt[:, g % 2].rearrange("p u r -> p (u r)").bitcast(BF16)
+            nc.vector.tensor_tensor(
+                out=xg[i][:, 512 * g : 512 * (g + 1)].rearrange("p (r u e) -> p r u e", u=2, e=2),
+                in0=src.rearrange("p (u r e) -> p r u e", u=2, e=2),
+                in1=xs[:, g].rearrange("p (u e) -> p u e", u=2).unsqueeze(1).to_broadcast([P, P, 2, 2]),
+                op=MUL,
+            )
+
+        xp = keep.tile([P, GA, 4, P], BF16, name="xp", align_bytes=64)
+
+        def plane_x(i, g):
+            pt = trx[i, g // 2]
+            for t in range(4):
+                u, e = divmod(t, 2)
+                nc.scalar.activation(
+                    out=xp[:, g, t, :],
+                    in_=pt[:, g % 2, u, :].bitcast(BF16)[:, e::2],
+                    func=ACT.Copy,
+                    scale=xs[:, g, t : t + 1],
+                )
+
+        def weave_x(i, g0, g1):
+            for g in range(g0, g1):
+                nc.gpsimd.tensor_scalar(
+                    out=xg[i][:, 512 * g : 512 * (g + 1)].rearrange("p (r t) -> p r t", t=4),
+                    in0=xp[:, g].rearrange("p t r -> p r t"),
+                    scalar1=1.0,
+                    scalar2=0.0,
+                    op0=MUL,
+                    op1=ADD,
+                )
+
+        def quant_x(i, g0, g1):
+            nc.vector.quantize_mx(
+                out=xq[i][:, P * g0 : P * g1].bitcast(FP8X4),
+                scales=xqs[i][:, P * g0 : P * g1],
+                in_=xg[i][:, 512 * g0 : 512 * g1],
+            )
+
+        acc = {}
+
+        def mm_a(i, n, b):
+            t = bank(b, [P, 512], F32, "c%d_%d" % (i, n))
+            acc[i, n] = t
+            for g in range(GA):
+                nc.tensor.matmul_mx(
+                    out=t[:],
+                    lhsT=xq[i][:, P * g : P * (g + 1)].bitcast(FP8X4),
+                    lhsT_scale=xqs[i][:, P * g : P * (g + 1)],
+                    rhs=wa[n][:, g].bitcast(FP8X4),
+                    rhs_scale=was[4 * g : P, 512 * n : 512 * (n + 1)],
+                    start=(g == 0),
+                    stop=(g == GA - 1),
+                )
+
+        def square(i, n):
+            junk = work.tile([P, 512], BF16, name="junk", bufs=2)
+            nc.scalar.activation(out=junk[:], in_=acc[i, n][:], func=ACT.Square, accum_out=ssq[i][:, n : n + 1])
+
+        def rms_a(i):
+            nc.scalar.activation(out=rms[i][:, 4:7], in_=ssq[i][:, 0:3], func=ACT.Copy, accum_out=rms[i][:, 0:1])
+            nc.scalar.activation(out=rms[i][:, 2:3], in_=rms[i][:, 0:1], func=ACT.Sqrt, scale=1.0 / RQ, bias=EPS)
+
+        def rms_b(i):
+            nc.vector.reciprocal(out=rms[i][:, 3:4], in_=rms[i][:, 2:3])
+
+        def norm(i, n):
+            nc.vector.scalar_tensor_tensor(
+                out=hb[i][:, 512 * n : 512 * (n + 1)],
+                in0=acc[i, n][:],
+                scalar=rms[i][:, 3:4],
+                in1=gbc[:, 512 * n : 512 * (n + 1)],
+                op0=MUL,
+                op1=MUL,
+            )
+
+        hs = {}
+
+        def norm_s(i, n):
+            t = work.tile([P, 512], F32, name="hs", bufs=3)
+            hs[i, n] = t
+            nc.scalar.activation(out=t[:], in_=acc[i, n][:], func=ACT.Copy, scale=rms[i][:, 3:4])
+
+        def norm_g(i, n):
+            nc.gpsimd.tensor_tensor(out=hb[i][:, 512 * n : 512 * (n + 1)], in0=hs[i, n][:], in1=gbc[:, 512 * n : 512 * (n + 1)], op=MUL)
+
+        trh = {}
+
+        def turn_h(i, part, b):
+            words = hb[i][:].bitcast(F32)
+            pt = bank(b, [P, 2, 2, P], F32, "trh%d_%d" % (i, part))
+            trh[i, part] = pt
+            for g in range(2 * part, min(2 * part + 2, GB)):
+                for u in range(2):
+                    nc.tensor.transpose(pt[:, g - 2 * part, u, :], words[:, 256 * g + u : 256 * (g + 1) : 2], ident[:])
+
+        def copy_h(i, part):
+            n = 2 - part
+            c0 = 1024 * part
+            nc.scalar.copy(
+                out=hg[i][:, c0 : c0 + 512 * n].bitcast(F32).rearrange("p (g r u) -> p g r u", g=n, u=2),
+                in_=trh[i, part][:, 0:n].rearrange("p g u r -> p g r u"),
+            )
+
+        def quant_h(i, part):
+            n = 2 - part
+            c0 = 256 * part
+            nc.vector.quantize_mx(
+                out=hq[i][:, c0 : c0 + P * n].bitcast(FP8X4),
+                scales=hqs[i][:, c0 : c0 + P * n],
+                in_=hg[i][:, 4 * c0 : 4 * c0 + 512 * n],
+            )
+
+        qacc = {}
+
+        def mm_b(i, n, b):
+            t = bank(b, [P, 512], F32, "q%d_%d" % (i, n))
+            qacc[i, n] = t
+            for g in range(GB):
+                nc.tensor.matmul_mx(
+                    out=t[:],
+                    lhsT=hq[i][:, P * g : P * (g + 1)].bitcast(FP8X4),
+                    lhsT_scale=hqs[i][:, P * g : P * (g + 1)],
+                    rhs=wb[n][:, g].bitcast(FP8X4),
+                    rhs_scale=wbs[4 * g : P, 512 * n : 512 * (n + 1)],
+                    start=(g == 0),
+                    stop=(g == GB - 1),
+                )
+
+        NOPE0 = (0, 1, 2)
+
+        def nope(i, n):
+            kind = n % 3
+            blk = qacc[i, n][:].rearrange("p (k c) -> p k c", c=64)[:, NOPE0[kind] :: 3, :]
+            h0 = 8 * (n // 3) + (0, 3, 6)[kind]
+            cnt = (3, 3, 2)[kind]
+            b, par = divmod(i, 2)
+            nc.scalar.copy(out=osb[b][:, h0 : h0 + cnt, par, 0:DN], in_=blk)
+
+        prod = {}
+
+        def rope_mul(i, n):
+            kind = n % 3
+            b, par = divmod(i, 2)
+            width = (320, 320, 384)[kind]
+            t = work.tile([P, 2, 384], F32, name="prod", bufs=6)
+            prod[i, n] = t
+            q = qacc[i, n]
+            runs = (
+                ((64, 2, 128, 0, 0), (448, 1, 64, 0, 256)),
+                ((0, 1, 64, 64, 0), (128, 2, 128, 0, 64)),
+                ((0, 2, 128, 0, 0), (384, 1, 128, 0, 256)),
+            )[kind]
+            for c0, cnt, w, t0, o0 in runs:
+                if cnt == 2:
+                    src = q[:, c0 : c0 + 384].rearrange("p (k c) -> p k c", c=192)[:, :, 0:w]
+                else:
+                    src = q[:, c0 : c0 + w].rearrange("p (k c) -> p k c", k=1)
+                nc.vector.tensor_tensor(
+                    out=t[:, :, o0 : o0 + cnt * w].rearrange("p o (k c) -> p o k c", k=cnt),
+                    in0=src.unsqueeze(1).to_broadcast([P, 2, cnt, w]),
+                    in1=tab[:, par, :, t0 : t0 + w].unsqueeze(2).to_broadcast([P, 2, cnt, w]),
+                    op=MUL,
+                )
+
+        def rope_add(i, n, eng):
+            kind = n % 3
+            b, par = divmod(i, 2)
+            t = prod[i, n]
+            base = 8 * (n // 3)
+            runs = (
+                ((0, 2, 64, 128, 0), (2, 1, 64, 64, 256)),
+                ((2, 1, 128, 64, 0), (3, 2, 64, 128, 64)),
+                ((5, 3, 64, 128, 0),),
+            )[kind]
+            for h0, cnt, f0, w, o0 in runs:
+                dst = osb[b][:, base + h0 : base + h0 + cnt, par, f0 : f0 + w].rearrange("p k (i two) -> p k i two", two=2)
+                a = t[:, 0, o0 : o0 + cnt * w].rearrange("p (k i two) -> p k i two", k=cnt, two=2)
+                s = t[:, 1, o0 : o0 + cnt * w].rearrange("p (k i two) -> p k i two", k=cnt, two=2)[:, :, :, ::-1]
+                eng.tensor_tensor(out=dst, in0=a, in1=s, op=ADD)
+
+        def store_one(i, n):
+            h0 = 8 * (n // 3) + (0, 2, 5)[n % 3]
+            cnt = (2, 3, 3)[n % 3]
+            b, par = divmod(i, 2)
+            nc.sync.dma_start(
+                out=out[b].rearrange("h (p two) d -> p h two d", two=2)[:, h0 : h0 + cnt, par, :],
+                in_=osb[b][:, h0 : h0 + cnt, par, :],
+            )
+
+        def store(b, n):
+            h0 = 8 * (n // 3) + (0, 2, 5)[n % 3]
+            cnt = (2, 3, 3)[n % 3]
+            nc.sync.dma_start(
+                out=out[b].rearrange("h (p two) d -> p h (two d)", two=2)[:, h0 : h0 + cnt, :],
+                in_=osb[b][:, h0 : h0 + cnt].rearrange("p h two d -> p h (two d)"),
+            )
+
+        cast_s(0, 1024, 1536)
+        cast_v(0, 0, 512)
+        cast_v(0, 512, 1024)
+        cast_s(0, 1536, 2048)
+        turn_x(0, 0, 0)
+        cast_s(1, 0, 1024)
+        turn_x(0, 1, 1)
+        scale_x(0, 1)
+        scale_x(0, 2)
+        turn_x(1, 0, 2)
+        scale_x(0, 3)
+        cast_s(1, 1024, 2048)
+        scale_x(1, 1)
+        scale_x(0, 0)
+        turn_x(1, 1, 3)
+        quant_x(0, 2, 4)
+        quant_x(0, 0, 2)
+        scale_x(1, 2)
+        mm_a(0, 0, 4)
+        scale_x(1, 3)
+        scale_x(1, 0)
+        mm_a(0, 1, 5)
+        square(0, 0)
+        quant_x(1, 0, 4)
+        mm_a(0, 2, 6)
+        square(0, 1)
+        cast_g(2, 0, 1024)
+        mm_a(1, 2, 7)
+        square(0, 2)
+        cast_g(2, 1024, 2048)
+        rms_a(0)
+        mm_a(1, 0, 1)
+        rms_b(0)
+        square(1, 2)
+        norm(0, 0)
+        cast_g(3, 0, 1024)
+        norm_s(0, 2)
+        norm(0, 1)
+        turn_x(2, 1, 0)
+        square(1, 0)
+        turn_x(2, 0, 3)
+        norm_g(0, 2)
+        scale_x(2, 2)
+        turn_x(3, 0, 2)
+        scale_x(2, 0)
+        turn_h(0, 0, 4)
+        cast_g(3, 1024, 2048)
+        plane_x(3, 0)
+        scale_x(2, 3)
+        turn_h(0, 1, 6)
+        mm_a(1, 1, 5)
+        plane_x(3, 1)
+        scale_x(2, 1)
+        weave_x(3, 0, 1)
+        copy_h(0, 1)
+        quant_x(2, 0, 4)
+        weave_x(3, 1, 2)
+        copy_h(0, 0)
+        turn_x(3, 1, 0)
+        quant_h(0, 1)
+        square(1, 1)
+        quant_h(0, 0)
+        mm_a(2, 1, 3)
+        plane_x(3, 3)
+        plane_x(3, 2)
+        mm_b(0, 0, 2)
+        weave_x(3, 3, 4)
+        square(2, 1)
+        weave_x(3, 2, 3)
+        mm_b(0, 2, 6)
+        rope_mul(0, 0)
+        rms_a(1)
+        mm_b(0, 1, 4)
+        rms_b(1)
+        nope(0, 2)
+        quant_x(3, 0, 4)
+        rope_add(0, 0, nc.gpsimd)
+        nope(0, 0)
+        norm_s(1, 2)
+        mm_b(0, 4, 0)
+        norm(1, 0)
+        nope(0, 1)
+        norm_g(1, 2)
+        norm(1, 1)
+        mm_a(3, 2, 2)
+        nope(0, 4)
+        rope_mul(0, 1)
+        mm_b(0, 5, 7)
+        rope_mul(0, 4)
+        rope_add(0, 1, nc.gpsimd)
+        square(3, 2)
+        rope_mul(0, 2)
+        mm_a(2, 0, 1)
+        rope_add(0, 4, nc.gpsimd)
+        nope(0, 5)
+        rope_mul(0, 5)
+        rope_add(0, 2, nc.gpsimd)
+        mm_a(2, 2, 5)
+        square(2, 0)
+        rope_add(0, 5, nc.gpsimd)
+        mm_b(0, 3, 4)
+        square(2, 2)
+        mm_a(3, 0, 0)
+        rms_a(2)
+        rope_mul(0, 3)
+        rms_b(2)
+        nope(0, 3)
+        turn_h(1, 1, 6)
+        rope_add(0, 3, nc.gpsimd)
+        norm(2, 0)
+        norm_s(2, 2)
+        turn_h(1, 0, 7)
+        norm(2, 1)
+        copy_h(1, 1)
+        mm_a(3, 1, 4)
+        norm_g(2, 2)
+        copy_h(1, 0)
+        quant_h(1, 1)
+        square(3, 0)
+        quant_h(1, 0)
+        turn_h(2, 0, 1)
+        square(3, 1)
+        mm_b(1, 2, 5)
+        copy_h(2, 0)
+        rms_a(3)
+        mm_b(1, 3, 6)
+        quant_h(2, 0)
+        nope(1, 2)
+        rms_b(3)
+        rope_mul(1, 2)
+        norm_s(3, 2)
+        mm_b(1, 0, 3)
+        nope(1, 3)
+        norm_g(3, 2)
+        norm(3, 0)
+        mm_b(1, 1, 7)
+        nope(1, 0)
+        rope_mul(1, 3)
+        rope_add(1, 2, nc.gpsimd)
+        turn_h(2, 1, 1)
+        nope(1, 1)
+        rope_mul(1, 0)
+        turn_h(3, 1, 2)
+        copy_h(2, 1)
+        mm_b(1, 4, 5)
+        copy_h(3, 1)
+        rope_add(1, 3, nc.gpsimd)
+        rope_mul(1, 1)
+        store(0, 2)
+        mm_b(1, 5, 0)
+        rope_add(1, 0, nc.gpsimd)
+        nope(1, 4)
+        quant_h(2, 1)
+        store(0, 3)
+        quant_h(3, 1)
+        norm(3, 1)
+        mm_b(2, 1, 6)
+        rope_add(1, 1, nc.gpsimd)
+        nope(1, 5)
+        store(0, 0)
+        rope_mul(1, 4)
+        mm_b(2, 4, 1)
+        store(0, 1)
+        nope(2, 1)
+        rope_mul(1, 5)
+        rope_add(1, 4, nc.gpsimd)
+        turn_h(3, 0, 3)
+        nope(2, 4)
+        rope_mul(2, 1)
+        rope_add(1, 5, nc.gpsimd)
+        store(0, 4)
+        mm_b(2, 0, 2)
+        copy_h(3, 0)
+        rope_mul(2, 4)
+        rope_add(2, 1, nc.gpsimd)
+        mm_b(2, 5, 7)
+        store(0, 5)
+        nope(2, 0)
+        quant_h(3, 0)
+        rope_add(2, 4, nc.gpsimd)
+        rope_mul(2, 0)
+        mm_b(2, 3, 4)
+        nope(2, 5)
+        rope_mul(2, 5)
+        rope_add(2, 0, nc.gpsimd)
+        mm_b(3, 0, 5)
+        nope(2, 3)
+        rope_mul(2, 3)
+        mm_b(3, 3, 0)
+        rope_add(2, 5, nc.gpsimd)
+        nope(3, 0)
+        rope_mul(3, 0)
+        mm_b(3, 1, 6)
+        rope_add(2, 3, nc.gpsimd)
+        nope(3, 3)
+        store_one(2, 5)
+        rope_mul(3, 3)
+        mm_b(3, 4, 3)
+        rope_add(3, 0, nc.gpsimd)
+        nope(3, 1)
+        rope_mul(3, 1)
+        rope_add(3, 3, nc.gpsimd)
+        mm_b(3, 2, 1)
+        store(1, 0)
+        nope(3, 4)
+        rope_mul(3, 4)
+        rope_add(3, 1, nc.gpsimd)
+        mm_b(3, 5, 2)
+        store(1, 3)
+        nope(3, 2)
+        rope_mul(3, 2)
+        rope_add(3, 4, nc.gpsimd)
+        mm_b(2, 2, 7)
+        store(1, 1)
+        nope(3, 5)
+        rope_mul(3, 5)
+        rope_add(3, 2, nc.gpsimd)
+        store(1, 4)
+        nope(2, 2)
+        rope_mul(2, 2)
+        rope_add(3, 5, nc.vector)
+        rope_add(2, 2, nc.gpsimd)
+        store_one(3, 5)
+        store(1, 2)

@@ -27,7 +27,8 @@ AX = mybir.AxisListType
 
 GA = D // 512
 GB = RQ // 512
-NB = NQ // 512
+NB = H // 2
+WB = 2 * DH
 
 
 def tile_multiheadlatentattention_pa_w8_kernel(
@@ -52,10 +53,11 @@ def tile_multiheadlatentattention_pa_w8_kernel(
         ssq = [keep.tile([P, 8], F32, name="ssq_%d" % (i,)) for i in range(4)]
         rms = [keep.tile([P, 8], F32, name="rms_%d" % (i,)) for i in range(4)]
         wa = [keep.tile([P, GA, 512], U32, name="wa_%d" % (i,), align_bytes=64) for i in range(GB)]
-        wb = [keep.tile([P, GB, 512], U32, name="wb_%d" % (i,), align_bytes=64) for i in range(NB)]
+        wb = [keep.tile([P, GB, 2 * WB], U32, name="wb_%d" % (i,), align_bytes=64) for i in range(NB // 2)]
         was = keep.tile([P, RQ], U8, name="was", align_bytes=64)
         wbs = keep.tile([P, NQ], U8, name="wbs", align_bytes=64)
         xs = keep.tile([P, GA, 4], F32, name="xs")
+        gz = keep.tile([P, RQ], BF16, name="gz", align_bytes=64)
         gbc = keep.tile([P, RQ], BF16, name="gbc", align_bytes=64)
         ones = keep.tile([P, P], BF16, name="ones", align_bytes=64)
         ident = keep.tile([P, P], F32, name="ident", align_bytes=64)
@@ -65,6 +67,7 @@ def tile_multiheadlatentattention_pa_w8_kernel(
         frac = keep.tile([P, 2, 2, 64], F32, name="frac")
         tab = keep.tile([P, 2, 2, P], F32, name="tab")
         warm = keep.tile([P, 1], F32, name="warm")
+        one32 = keep.tile([P, 1], F32, name="one32")
         osb = [keep.tile([P, H, 2, DH], F32, name="osb_%d" % (i,)) for i in range(2)]
 
         def bank(i, shape, dtype, name):
@@ -74,7 +77,9 @@ def tile_multiheadlatentattention_pa_w8_kernel(
         make_identity(nc, ident[:])
         nc.gpsimd.memset(wbs[:].bitcast(I32), 0)
         nc.vector.memset(was[:].bitcast(I32), 0)
+        nc.vector.memset(gz[:], 0.0)
         nc.vector.memset(ones[:], 1.0)
+        nc.vector.memset(one32[:], 1.0)
 
         def load_x(i):
             b, par = divmod(i, 2)
@@ -90,12 +95,14 @@ def tile_multiheadlatentattention_pa_w8_kernel(
                 )
 
         def load_w(tile, dram, n):
+            w = tile.shape[2]
             nc.sync.dma_start(
                 out=tile[:].bitcast(I32),
-                in_=dram.rearrange("g p n t -> p g (n t)")[:, :, 2048 * n : 2048 * (n + 1)].bitcast(I32),
+                in_=dram.rearrange("g p n t -> p g (n t)")[:, :, 4 * w * n : 4 * w * (n + 1)].bitcast(I32),
             )
 
         nc.scalar.dma_start(out=xs[:], in_=x_scale.rearrange("a b (g p t) -> p (a b g) t", p=P, t=4))
+        nc.scalar.dma_start(out=gz[0:1, :], in_=q_a_norm_w.unsqueeze(0))
         load_x(0)
         load_scales(was, Wqa_scales, GA)
         load_x(1)
@@ -104,10 +111,11 @@ def tile_multiheadlatentattention_pa_w8_kernel(
         load_w(wa[2], Wqa_words, 2)
         load_x(2)
         load_x(3)
-        nc.sync.dma_start(out=gbc[:], in_=q_a_norm_w.partition_broadcast(P))
         load_scales(wbs, Wqb_scales, GB)
-        for n in range(NB):
-            load_w(wb[n], Wqb_words, n)
+        load_w(wb[0], Wqb_words, 0)
+        load_w(wb[1], Wqb_words, 1)
+        load_w(wb[2], Wqb_words, 2)
+        load_w(wb[3], Wqb_words, 3)
 
         nc.vector.tensor_scalar(out=turns[:, :, 0:1], in0=pos[:].unsqueeze(2), scalar1=1.0 / (2.0 * math.pi), scalar2=None, op0=MUL)
         for j in range(6):
@@ -130,8 +138,19 @@ def tile_multiheadlatentattention_pa_w8_kernel(
         def cast_g(i, lo, hi):
             nc.gpsimd.tensor_copy(out=xb[i][:, lo:hi], in_=x8[i][:, lo:hi].bitcast(FP8))
 
+        sorted_x = set()
+
         def cast_v(i, lo, hi):
-            nc.vector.tensor_copy(out=xb[i][:, lo:hi], in_=x8[i][:, lo:hi].bitcast(FP8))
+            for c in range(lo, hi, 512):
+                nc.vector.tensor_scalar(
+                    out=xb[i][:, c : c + 512].rearrange("p (u q e) -> p q u e", u=2, e=2),
+                    in0=x8[i][:, c : c + 512].bitcast(FP8).rearrange("p (q u e) -> p q u e", u=2, e=2),
+                    scalar1=one32[:],
+                    scalar2=None,
+                    op0=MUL,
+                )
+                sorted_x.add((i, c // 512))
+
 
         trx = {}
 
@@ -141,7 +160,9 @@ def tile_multiheadlatentattention_pa_w8_kernel(
             words = xb[i][:].bitcast(F32)
             for g in (2 * half, 2 * half + 1):
                 for u in range(2):
-                    nc.tensor.transpose(pt[:, g - 2 * half, u, :], words[:, 256 * g + u : 256 * (g + 1) : 2], ident[:])
+                    w0 = 256 * g
+                    cols = slice(w0 + P * u, w0 + P * (u + 1)) if (i, g) in sorted_x else slice(w0 + u, w0 + 256, 2)
+                    nc.tensor.transpose(pt[:, g - 2 * half, u, :], words[:, cols], ident[:])
 
         def scale_x(i, g):
             pt = trx[i, g // 2]
@@ -211,22 +232,31 @@ def tile_multiheadlatentattention_pa_w8_kernel(
         def rms_b(i):
             nc.vector.reciprocal(out=rms[i][:, 3:4], in_=rms[i][:, 2:3])
 
+        by_word = "p (q u e) -> p u q e"
+
         def norm(i, n):
-            nc.vector.scalar_tensor_tensor(
-                out=hb[i][:, 512 * n : 512 * (n + 1)],
-                in0=acc[i, n][:],
-                scalar=rms[i][:, 3:4],
-                in1=gbc[:, 512 * n : 512 * (n + 1)],
-                op0=MUL,
-                op1=MUL,
-            )
+            for u in range(2):
+                cols = slice(512 * n + 256 * u, 512 * n + 256 * (u + 1))
+                nc.vector.scalar_tensor_tensor(
+                    out=hb[i][:, cols].rearrange("p (q e) -> p q e", e=2),
+                    in0=acc[i, n][:].rearrange(by_word, u=2, e=2)[:, u],
+                    scalar=rms[i][:, 3:4],
+                    in1=gbc[:, cols].rearrange("p (q e) -> p q e", e=2),
+                    op0=MUL,
+                    op1=MUL,
+                )
 
         hs = {}
 
         def norm_s(i, n):
             t = work.tile([P, 512], F32, name="hs", bufs=3)
             hs[i, n] = t
-            nc.scalar.activation(out=t[:], in_=acc[i, n][:], func=ACT.Copy, scale=rms[i][:, 3:4])
+            nc.scalar.activation(
+                out=t[:].rearrange("p (u q e) -> p u q e", u=2, e=2),
+                in_=acc[i, n][:].rearrange(by_word, u=2, e=2),
+                func=ACT.Copy,
+                scale=rms[i][:, 3:4],
+            )
 
         def norm_g(i, n):
             nc.gpsimd.tensor_tensor(out=hb[i][:, 512 * n : 512 * (n + 1)], in0=hs[i, n][:], in1=gbc[:, 512 * n : 512 * (n + 1)], op=MUL)
@@ -239,12 +269,14 @@ def tile_multiheadlatentattention_pa_w8_kernel(
             trh[i, part] = pt
             for g in range(2 * part, min(2 * part + 2, GB)):
                 for u in range(2):
-                    nc.tensor.transpose(pt[:, g - 2 * part, u, :], words[:, 256 * g + u : 256 * (g + 1) : 2], ident[:])
+                    w0 = 256 * g + P * u
+                    nc.tensor.transpose(pt[:, g - 2 * part, u, :], words[:, w0 : w0 + P], ident[:])
 
-        def copy_h(i, part):
+        def copy_h(i, part, eng=None):
             n = 2 - part
             c0 = 1024 * part
-            nc.scalar.copy(
+            copy = nc.scalar.copy if eng is None else eng.tensor_copy
+            copy(
                 out=hg[i][:, c0 : c0 + 512 * n].bitcast(F32).rearrange("p (g r u) -> p g r u", g=n, u=2),
                 in_=trh[i, part][:, 0:n].rearrange("p g u r -> p g r u"),
             )
@@ -261,309 +293,335 @@ def tile_multiheadlatentattention_pa_w8_kernel(
         qacc = {}
 
         def mm_b(i, n, b):
-            t = bank(b, [P, 512], F32, "q%d_%d" % (i, n))
+            t = bank(b, [P, WB], F32, "q%d_%d" % (i, n))
             qacc[i, n] = t
-            for g in range(GB):
-                nc.tensor.matmul_mx(
-                    out=t[:],
-                    lhsT=hq[i][:, P * g : P * (g + 1)].bitcast(FP8X4),
-                    lhsT_scale=hqs[i][:, P * g : P * (g + 1)],
-                    rhs=wb[n][:, g].bitcast(FP8X4),
-                    rhs_scale=wbs[4 * g : P, 512 * n : 512 * (n + 1)],
-                    start=(g == 0),
-                    stop=(g == GB - 1),
-                )
-
-        NOPE0 = (0, 1, 2)
+            for c0, c1 in ((0, 256), (256, WB)):
+                for g in range(GB):
+                    nc.tensor.matmul_mx(
+                        out=t[:, c0:c1],
+                        lhsT=hq[i][:, P * g : P * (g + 1)].bitcast(FP8X4),
+                        lhsT_scale=hqs[i][:, P * g : P * (g + 1)],
+                        rhs=wb[n // 2][:, g, WB * (n % 2) + c0 : WB * (n % 2) + c1].bitcast(FP8X4),
+                        rhs_scale=wbs[4 * g : P, WB * n + c0 : WB * n + c1],
+                        start=(g == 0),
+                        stop=(g == GB - 1),
+                    )
 
         def nope(i, n):
-            kind = n % 3
-            blk = qacc[i, n][:].rearrange("p (k c) -> p k c", c=64)[:, NOPE0[kind] :: 3, :]
-            h0 = 8 * (n // 3) + (0, 3, 6)[kind]
-            cnt = (3, 3, 2)[kind]
             b, par = divmod(i, 2)
-            nc.scalar.copy(out=osb[b][:, h0 : h0 + cnt, par, 0:DN], in_=blk)
+            nc.scalar.copy(
+                out=osb[b][:, 2 * n : 2 * n + 2, par, 0:DN],
+                in_=qacc[i, n][:].rearrange("p (h d) -> p h d", h=2)[:, :, 0:DN],
+            )
 
         prod = {}
 
         def rope_mul(i, n):
-            kind = n % 3
-            b, par = divmod(i, 2)
-            width = (320, 320, 384)[kind]
-            t = work.tile([P, 2, 384], F32, name="prod", bufs=6)
+            t = work.tile([P, 2, 2, DR], F32, name="prod", bufs=8)
             prod[i, n] = t
-            q = qacc[i, n]
-            runs = (
-                ((64, 2, 128, 0, 0), (448, 1, 64, 0, 256)),
-                ((0, 1, 64, 64, 0), (128, 2, 128, 0, 64)),
-                ((0, 2, 128, 0, 0), (384, 1, 128, 0, 256)),
-            )[kind]
-            for c0, cnt, w, t0, o0 in runs:
-                if cnt == 2:
-                    src = q[:, c0 : c0 + 384].rearrange("p (k c) -> p k c", c=192)[:, :, 0:w]
-                else:
-                    src = q[:, c0 : c0 + w].rearrange("p (k c) -> p k c", k=1)
-                nc.vector.tensor_tensor(
-                    out=t[:, :, o0 : o0 + cnt * w].rearrange("p o (k c) -> p o k c", k=cnt),
-                    in0=src.unsqueeze(1).to_broadcast([P, 2, cnt, w]),
-                    in1=tab[:, par, :, t0 : t0 + w].unsqueeze(2).to_broadcast([P, 2, cnt, w]),
-                    op=MUL,
-                )
+            nc.vector.tensor_tensor(
+                out=t[:],
+                in0=qacc[i, n][:].rearrange("p (h d) -> p h d", h=2)[:, :, DN:DH].unsqueeze(1).to_broadcast([P, 2, 2, DR]),
+                in1=tab[:, i % 2].unsqueeze(2).to_broadcast([P, 2, 2, DR]),
+                op=MUL,
+            )
 
         def rope_add(i, n, eng):
-            kind = n % 3
             b, par = divmod(i, 2)
             t = prod[i, n]
-            base = 8 * (n // 3)
-            runs = (
-                ((0, 2, 64, 128, 0), (2, 1, 64, 64, 256)),
-                ((2, 1, 128, 64, 0), (3, 2, 64, 128, 64)),
-                ((5, 3, 64, 128, 0),),
-            )[kind]
-            for h0, cnt, f0, w, o0 in runs:
-                dst = osb[b][:, base + h0 : base + h0 + cnt, par, f0 : f0 + w].rearrange("p k (i two) -> p k i two", two=2)
-                a = t[:, 0, o0 : o0 + cnt * w].rearrange("p (k i two) -> p k i two", k=cnt, two=2)
-                s = t[:, 1, o0 : o0 + cnt * w].rearrange("p (k i two) -> p k i two", k=cnt, two=2)[:, :, :, ::-1]
-                eng.tensor_tensor(out=dst, in0=a, in1=s, op=ADD)
-
-        def store_one(i, n):
-            h0 = 8 * (n // 3) + (0, 2, 5)[n % 3]
-            cnt = (2, 3, 3)[n % 3]
-            b, par = divmod(i, 2)
-            nc.sync.dma_start(
-                out=out[b].rearrange("h (p two) d -> p h two d", two=2)[:, h0 : h0 + cnt, par, :],
-                in_=osb[b][:, h0 : h0 + cnt, par, :],
+            pairs = "p h (i two) -> p h i two"
+            eng.tensor_tensor(
+                out=osb[b][:, 2 * n : 2 * n + 2, par, DN:DH].rearrange(pairs, two=2),
+                in0=t[:, 0].rearrange(pairs, two=2),
+                in1=t[:, 1].rearrange(pairs, two=2)[:, :, :, ::-1],
+                op=ADD,
             )
 
         def store(b, n):
-            h0 = 8 * (n // 3) + (0, 2, 5)[n % 3]
-            cnt = (2, 3, 3)[n % 3]
             nc.sync.dma_start(
-                out=out[b].rearrange("h (p two) d -> p h (two d)", two=2)[:, h0 : h0 + cnt, :],
-                in_=osb[b][:, h0 : h0 + cnt].rearrange("p h two d -> p h (two d)"),
+                out=out[b].rearrange("h (p two) d -> p h (two d)", two=2)[:, 2 * n : 2 * n + 2, :],
+                in_=osb[b][:, 2 * n : 2 * n + 2].rearrange("p h two d -> p h (two d)"),
             )
 
-        cast_s(0, 1024, 1536)
-        cast_v(0, 0, 512)
-        cast_v(0, 512, 1024)
-        cast_s(0, 1536, 2048)
-        turn_x(0, 0, 0)
-        cast_s(1, 0, 1024)
-        turn_x(0, 1, 1)
-        scale_x(0, 1)
-        scale_x(0, 2)
-        turn_x(1, 0, 2)
-        scale_x(0, 3)
-        cast_s(1, 1024, 2048)
-        scale_x(1, 1)
+        def store_one(i, n):
+            b, par = divmod(i, 2)
+            nc.sync.dma_start(
+                out=out[b].rearrange("h (p two) d -> p h two d", two=2)[:, 2 * n : 2 * n + 2, par, :],
+                in_=osb[b][:, 2 * n : 2 * n + 2, par, :],
+            )
+
+        gain_ps = {}
+
+        def gain_mm(n, b):
+            gp = bank(b, [P, 512], F32, "gain%d" % (n,))
+            gain_ps[n] = gp
+            nc.tensor.matmul(gp[:], ones[:], gz[:, 512 * n : 512 * (n + 1)], start=True, stop=True)
+
+        def gain_copy(n):
+            nc.scalar.copy(
+                out=gbc[:, 512 * n : 512 * (n + 1)].rearrange("p (u q e) -> p u q e", u=2, e=2),
+                in_=gain_ps[n][:].rearrange(by_word, u=2, e=2),
+            )
+
+        gain_mm(0, 0)
+        cast_v(0, 0, 1024)
+        cast_s(0, 1024, 2048)
+        gain_mm(1, 1)
+        gain_mm(2, 2)
+        cast_v(1, 0, 1024)
+        turn_x(0, 0, 3)
+        gain_copy(0)
+        turn_x(0, 1, 4)
         scale_x(0, 0)
-        turn_x(1, 1, 3)
-        quant_x(0, 2, 4)
+        scale_x(0, 1)
+        cast_s(1, 1024, 2048)
+        turn_x(1, 0, 5)
+        scale_x(0, 2)
+        scale_x(0, 3)
+        plane_x(1, 0)
+        plane_x(1, 1)
+        turn_x(1, 1, 6)
         quant_x(0, 0, 2)
+        nc.scalar.activation(out=warm[:], in_=ones[:, 0:1], func=ACT.Sqrt)
+        quant_x(0, 2, 4)
+        weave_x(1, 0, 2)
         scale_x(1, 2)
-        mm_a(0, 0, 4)
         scale_x(1, 3)
-        scale_x(1, 0)
-        mm_a(0, 1, 5)
-        square(0, 0)
+        mm_a(0, 0, 7)
+        gain_copy(2)
+        mm_a(0, 1, 0)
         quant_x(1, 0, 4)
-        mm_a(0, 2, 6)
+        square(0, 0)
+        gain_copy(1)
+        mm_a(1, 0, 3)
         square(0, 1)
-        cast_g(2, 0, 1024)
-        mm_a(1, 2, 7)
-        square(0, 2)
-        cast_g(2, 1024, 2048)
-        rms_a(0)
-        mm_a(1, 0, 1)
-        rms_b(0)
-        square(1, 2)
-        norm(0, 0)
-        cast_g(3, 0, 1024)
-        norm_s(0, 2)
-        norm(0, 1)
-        turn_x(2, 1, 0)
+        cast_v(2, 0, 1024)
+        cast_s(2, 1024, 2048)
+        mm_a(0, 2, 4)
+        cast_v(3, 0, 1024)
         square(1, 0)
-        turn_x(2, 0, 3)
-        norm_g(0, 2)
-        scale_x(2, 2)
-        turn_x(3, 0, 2)
+        cast_v(3, 1024, 2048)
+        turn_x(2, 0, 5)
+        turn_x(2, 1, 6)
+        square(0, 2)
         scale_x(2, 0)
-        turn_h(0, 0, 4)
-        cast_g(3, 1024, 2048)
-        plane_x(3, 0)
-        scale_x(2, 3)
-        turn_h(0, 1, 6)
-        mm_a(1, 1, 5)
-        plane_x(3, 1)
         scale_x(2, 1)
-        weave_x(3, 0, 1)
-        copy_h(0, 1)
+        mm_a(1, 2, 2)
+        rms_a(0)
+        scale_x(2, 2)
+        scale_x(2, 3)
+        mm_a(1, 1, 1)
+        square(1, 2)
+        rms_b(0)
         quant_x(2, 0, 4)
-        weave_x(3, 1, 2)
-        copy_h(0, 0)
-        turn_x(3, 1, 0)
-        quant_h(0, 1)
+        norm_s(0, 2)
+        turn_x(3, 0, 5)
+        turn_x(3, 1, 6)
+        norm(0, 1)
         square(1, 1)
-        quant_h(0, 0)
-        mm_a(2, 1, 3)
-        plane_x(3, 3)
-        plane_x(3, 2)
-        mm_b(0, 0, 2)
-        weave_x(3, 3, 4)
-        square(2, 1)
-        weave_x(3, 2, 3)
-        mm_b(0, 2, 6)
-        rope_mul(0, 0)
+        norm_g(0, 2)
+        mm_a(2, 1, 4)
+        scale_x(3, 2)
+        scale_x(3, 3)
+        plane_x(3, 0)
+        plane_x(3, 1)
+        mm_a(2, 2, 0)
+        norm(0, 0)
         rms_a(1)
-        mm_b(0, 1, 4)
+        weave_x(3, 0, 2)
+        square(2, 1)
+        mm_a(2, 0, 6)
         rms_b(1)
-        nope(0, 2)
-        quant_x(3, 0, 4)
-        rope_add(0, 0, nc.gpsimd)
-        nope(0, 0)
-        norm_s(1, 2)
-        mm_b(0, 4, 0)
-        norm(1, 0)
-        nope(0, 1)
-        norm_g(1, 2)
         norm(1, 1)
-        mm_a(3, 2, 2)
-        nope(0, 4)
-        rope_mul(0, 1)
-        mm_b(0, 5, 7)
-        rope_mul(0, 4)
-        rope_add(0, 1, nc.gpsimd)
-        square(3, 2)
-        rope_mul(0, 2)
-        mm_a(2, 0, 1)
-        rope_add(0, 4, nc.gpsimd)
-        nope(0, 5)
-        rope_mul(0, 5)
-        rope_add(0, 2, nc.gpsimd)
-        mm_a(2, 2, 5)
-        square(2, 0)
-        rope_add(0, 5, nc.gpsimd)
-        mm_b(0, 3, 4)
         square(2, 2)
-        mm_a(3, 0, 0)
+        norm(1, 0)
+        turn_h(0, 1, 5)
+        square(2, 0)
+        turn_h(0, 0, 7)
+        quant_x(3, 0, 4)
+        turn_h(1, 0, 1)
+        copy_h(0, 1)
+        copy_h(0, 0, nc.vector)
         rms_a(2)
-        rope_mul(0, 3)
-        rms_b(2)
-        nope(0, 3)
-        turn_h(1, 1, 6)
-        rope_add(0, 3, nc.gpsimd)
-        norm(2, 0)
-        norm_s(2, 2)
-        turn_h(1, 0, 7)
-        norm(2, 1)
-        copy_h(1, 1)
-        mm_a(3, 1, 4)
-        norm_g(2, 2)
+        mm_a(3, 0, 3)
         copy_h(1, 0)
-        quant_h(1, 1)
-        square(3, 0)
+        quant_h(0, 1)
+        rms_b(2)
+        quant_h(0, 0)
+        norm_s(2, 1)
+        norm(2, 0)
+        mm_b(0, 1, 5)
+        norm_s(2, 2)
         quant_h(1, 0)
-        turn_h(2, 0, 1)
+        mm_a(3, 2, 7)
+        norm(1, 2)
+        norm_g(2, 1)
+        square(3, 0)
+        rope_mul(0, 1)
+        mm_b(0, 4, 1)
+        norm_g(2, 2)
+        square(3, 2)
+        mm_b(0, 2, 4)
+        nope(0, 1)
+        rope_mul(0, 4)
+        mm_a(3, 1, 6)
+        rope_add(0, 1, nc.gpsimd)
+        rope_mul(0, 2)
+        nope(0, 4)
+        rope_add(0, 4, nc.gpsimd)
+        nope(0, 2)
+        turn_h(2, 1, 0)
         square(3, 1)
-        mm_b(1, 2, 5)
-        copy_h(2, 0)
+        turn_h(1, 1, 2)
+        rope_add(0, 2, nc.gpsimd)
+        mm_b(0, 0, 5)
+        copy_h(1, 1, nc.vector)
+        copy_h(2, 1)
         rms_a(3)
-        mm_b(1, 3, 6)
-        quant_h(2, 0)
-        nope(1, 2)
+        quant_h(1, 1)
+        mm_b(0, 7, 1)
+        quant_h(2, 1)
+        nope(0, 0)
         rms_b(3)
-        rope_mul(1, 2)
+        rope_mul(0, 0)
+        mm_b(1, 6, 4)
         norm_s(3, 2)
-        mm_b(1, 0, 3)
-        nope(1, 3)
-        norm_g(3, 2)
+        rope_mul(0, 7)
+        mm_b(1, 4, 2)
+        rope_add(0, 0, nc.gpsimd)
+        nope(1, 6)
         norm(3, 0)
-        mm_b(1, 1, 7)
+        nope(0, 7)
+        mm_b(1, 1, 0)
+        rope_add(0, 7, nc.gpsimd)
+        nope(1, 4)
+        norm(3, 1)
+        mm_b(1, 3, 5)
+        norm_g(3, 2)
+        nope(1, 1)
+        rope_mul(1, 4)
+        mm_b(1, 0, 7)
+        nope(1, 3)
+        rope_mul(1, 1)
+        rope_add(1, 4, nc.gpsimd)
+        mm_b(1, 2, 1)
         nope(1, 0)
         rope_mul(1, 3)
-        rope_add(1, 2, nc.gpsimd)
-        turn_h(2, 1, 1)
-        nope(1, 1)
-        rope_mul(1, 0)
-        turn_h(3, 1, 2)
-        copy_h(2, 1)
-        mm_b(1, 4, 5)
-        copy_h(3, 1)
-        rope_add(1, 3, nc.gpsimd)
-        rope_mul(1, 1)
-        store(0, 2)
-        mm_b(1, 5, 0)
-        rope_add(1, 0, nc.gpsimd)
-        nope(1, 4)
-        quant_h(2, 1)
-        store(0, 3)
-        quant_h(3, 1)
-        norm(3, 1)
-        mm_b(2, 1, 6)
         rope_add(1, 1, nc.gpsimd)
-        nope(1, 5)
-        store(0, 0)
-        rope_mul(1, 4)
-        mm_b(2, 4, 1)
-        store(0, 1)
-        nope(2, 1)
-        rope_mul(1, 5)
-        rope_add(1, 4, nc.gpsimd)
-        turn_h(3, 0, 3)
-        nope(2, 4)
-        rope_mul(2, 1)
-        rope_add(1, 5, nc.gpsimd)
+        turn_h(3, 1, 3)
         store(0, 4)
-        mm_b(2, 0, 2)
+        rope_mul(1, 0)
+        nope(1, 2)
+        turn_h(3, 0, 6)
+        copy_h(3, 1)
+        turn_h(2, 0, 2)
+        rope_add(1, 3, nc.gpsimd)
+        rope_mul(1, 2)
         copy_h(3, 0)
-        rope_mul(2, 4)
-        rope_add(2, 1, nc.gpsimd)
-        mm_b(2, 5, 7)
-        store(0, 5)
-        nope(2, 0)
+        store(0, 1)
+        mm_b(0, 3, 0)
+        rope_add(1, 0, nc.vector)
+        copy_h(2, 0)
+        mm_b(0, 6, 5)
         quant_h(3, 0)
-        rope_add(2, 4, nc.gpsimd)
-        rope_mul(2, 0)
-        mm_b(2, 3, 4)
-        nope(2, 5)
-        rope_mul(2, 5)
-        rope_add(2, 0, nc.gpsimd)
-        mm_b(3, 0, 5)
-        nope(2, 3)
-        rope_mul(2, 3)
-        mm_b(3, 3, 0)
-        rope_add(2, 5, nc.gpsimd)
-        nope(3, 0)
-        rope_mul(3, 0)
-        mm_b(3, 1, 6)
-        rope_add(2, 3, nc.gpsimd)
-        nope(3, 3)
-        store_one(2, 5)
-        rope_mul(3, 3)
+        store(0, 0)
+        nope(0, 3)
+        quant_h(3, 1)
+        quant_h(2, 0)
+        mm_b(1, 7, 7)
+        rope_mul(0, 3)
+        rope_add(1, 2, nc.gpsimd)
+        nope(0, 6)
         mm_b(3, 4, 3)
-        rope_add(3, 0, nc.gpsimd)
-        nope(3, 1)
-        rope_mul(3, 1)
-        rope_add(3, 3, nc.gpsimd)
-        mm_b(3, 2, 1)
-        store(1, 0)
+        rope_mul(0, 6)
+        nope(1, 7)
+        rope_add(0, 3, nc.gpsimd)
+        store(0, 2)
+        mm_b(2, 4, 1)
+        rope_mul(1, 7)
         nope(3, 4)
+        rope_add(0, 6, nc.gpsimd)
+        store(0, 3)
         rope_mul(3, 4)
-        rope_add(3, 1, nc.gpsimd)
-        mm_b(3, 5, 2)
-        store(1, 3)
-        nope(3, 2)
-        rope_mul(3, 2)
+        mm_b(3, 7, 6)
+        nope(2, 4)
+        rope_add(1, 7, nc.gpsimd)
+        rope_mul(2, 4)
+        mm_b(2, 3, 2)
+        nope(3, 7)
         rope_add(3, 4, nc.gpsimd)
+        rope_mul(1, 6)
+        store(0, 7)
+        mm_b(3, 0, 0)
+        nope(2, 3)
+        rope_add(2, 4, nc.gpsimd)
+        rope_mul(3, 7)
+        mm_b(3, 3, 5)
+        nope(3, 0)
+        rope_mul(2, 3)
+        rope_add(1, 6, nc.gpsimd)
+        mm_b(3, 6, 7)
+        store(1, 4)
+        nope(3, 3)
+        rope_mul(3, 0)
+        rope_add(3, 7, nc.gpsimd)
+        mm_b(2, 5, 3)
+        store(0, 6)
+        nope(3, 6)
+        rope_mul(3, 3)
+        rope_add(3, 0, nc.gpsimd)
+        mm_b(2, 1, 1)
+        rope_mul(3, 6)
+        nope(2, 5)
+        rope_add(2, 3, nc.gpsimd)
+        mm_b(2, 7, 4)
+        rope_mul(2, 5)
+        nope(2, 1)
+        rope_add(3, 3, nc.gpsimd)
+        mm_b(3, 1, 6)
+        rope_mul(2, 1)
+        nope(2, 7)
+        rope_add(2, 5, nc.gpsimd)
+        rope_mul(2, 7)
+        mm_b(2, 6, 2)
+        store(1, 3)
+        nope(3, 1)
+        rope_add(2, 1, nc.gpsimd)
+        rope_mul(3, 1)
+        mm_b(3, 5, 0)
+        nope(2, 6)
+        rope_add(2, 7, nc.vector)
+        mm_b(3, 2, 5)
+        nope(3, 5)
+        rope_add(3, 1, nc.vector)
+        store(1, 7)
+        rope_mul(3, 5)
+        rope_add(3, 6, nc.gpsimd)
         mm_b(2, 2, 7)
         store(1, 1)
-        nope(3, 5)
-        rope_mul(3, 5)
-        rope_add(3, 2, nc.gpsimd)
-        store(1, 4)
+        nope(3, 2)
+        rope_mul(2, 6)
+        mm_b(2, 0, 3)
+        rope_add(3, 5, nc.gpsimd)
         nope(2, 2)
+        rope_mul(3, 2)
+        mm_b(1, 5, 1)
+        rope_add(2, 6, nc.gpsimd)
+        nope(2, 0)
+        store(1, 5)
         rope_mul(2, 2)
-        rope_add(3, 5, nc.vector)
-        rope_add(2, 2, nc.gpsimd)
-        store_one(3, 5)
+        mm_b(0, 5, 4)
+        rope_add(3, 2, nc.gpsimd)
+        nope(1, 5)
+        rope_mul(2, 0)
+        store(1, 6)
+        nope(0, 5)
+        rope_add(2, 2, nc.vector)
+        rope_mul(0, 5)
+        rope_add(2, 0, nc.gpsimd)
         store(1, 2)
+        rope_mul(1, 5)
+        rope_add(0, 5, nc.gpsimd)
+        store(1, 0)
+        rope_add(1, 5, nc.vector)
+        store(0, 5)

@@ -76,9 +76,9 @@ def tile_multiheadlatentattention_pa_w8_kernel(
         nc.gpsimd.iota(pos[:], pattern=[[1, 2]], base=0, channel_multiplier=2)
         make_identity(nc, ident[:])
         nc.gpsimd.memset(wbs[:].bitcast(I32), 0)
+        nc.vector.memset(ones[:], 1.0)
         nc.vector.memset(was[:].bitcast(I32), 0)
         nc.vector.memset(gz[:], 0.0)
-        nc.vector.memset(ones[:], 1.0)
         nc.vector.memset(one32[:], 1.0)
 
         def load_x(i):
@@ -108,8 +108,8 @@ def tile_multiheadlatentattention_pa_w8_kernel(
         load_x(1)
         load_w(wa[0], Wqa_words, 0)
         load_w(wa[1], Wqa_words, 1)
-        load_w(wa[2], Wqa_words, 2)
         load_x(2)
+        load_w(wa[2], Wqa_words, 2)
         load_x(3)
         load_scales(wbs, Wqb_scales, GB)
         load_w(wb[0], Wqb_words, 0)
@@ -174,30 +174,6 @@ def tile_multiheadlatentattention_pa_w8_kernel(
                 op=MUL,
             )
 
-        xp = keep.tile([P, GA, 4, P], BF16, name="xp", align_bytes=64)
-
-        def plane_x(i, g):
-            pt = trx[i, g // 2]
-            for t in range(4):
-                u, e = divmod(t, 2)
-                nc.scalar.activation(
-                    out=xp[:, g, t, :],
-                    in_=pt[:, g % 2, u, :].bitcast(BF16)[:, e::2],
-                    func=ACT.Copy,
-                    scale=xs[:, g, t : t + 1],
-                )
-
-        def weave_x(i, g0, g1):
-            for g in range(g0, g1):
-                nc.gpsimd.tensor_scalar(
-                    out=xg[i][:, 512 * g : 512 * (g + 1)].rearrange("p (r t) -> p r t", t=4),
-                    in0=xp[:, g].rearrange("p t r -> p r t"),
-                    scalar1=1.0,
-                    scalar2=0.0,
-                    op0=MUL,
-                    op1=ADD,
-                )
-
         def quant_x(i, g0, g1):
             nc.vector.quantize_mx(
                 out=xq[i][:, P * g0 : P * g1].bitcast(FP8X4),
@@ -207,12 +183,12 @@ def tile_multiheadlatentattention_pa_w8_kernel(
 
         acc = {}
 
-        def mm_a(i, n, b):
-            t = bank(b, [P, 512], F32, "c%d_%d" % (i, n))
-            acc[i, n] = t
-            for g in range(GA):
+        def mm_a(i, n, b, groups=range(GA)):
+            if (i, n) not in acc:
+                acc[i, n] = bank(b, [P, 512], F32, "c%d_%d" % (i, n))
+            for g in groups:
                 nc.tensor.matmul_mx(
-                    out=t[:],
+                    out=acc[i, n][:],
                     lhsT=xq[i][:, P * g : P * (g + 1)].bitcast(FP8X4),
                     lhsT_scale=xqs[i][:, P * g : P * (g + 1)],
                     rhs=wa[n][:, g].bitcast(FP8X4),
@@ -326,16 +302,26 @@ def tile_multiheadlatentattention_pa_w8_kernel(
                 op=MUL,
             )
 
+        turned = {}
+        pairs = "p h (i two) -> p h i two"
+
+        def swap(i, n):
+            t = work.tile([P, 2, DR], F32, name="turned", bufs=4)
+            turned[i, n] = t
+            nc.scalar.copy(out=t[:].rearrange(pairs, two=2), in_=prod[i, n][:, 1].rearrange(pairs, two=2)[:, :, :, ::-1])
+
         def rope_add(i, n, eng):
             b, par = divmod(i, 2)
             t = prod[i, n]
-            pairs = "p h (i two) -> p h i two"
-            eng.tensor_tensor(
-                out=osb[b][:, 2 * n : 2 * n + 2, par, DN:DH].rearrange(pairs, two=2),
-                in0=t[:, 0].rearrange(pairs, two=2),
-                in1=t[:, 1].rearrange(pairs, two=2)[:, :, :, ::-1],
-                op=ADD,
-            )
+            if (i, n) in turned:
+                eng.tensor_tensor(out=osb[b][:, 2 * n : 2 * n + 2, par, DN:DH], in0=t[:, 0], in1=turned[i, n][:], op=ADD)
+            else:
+                eng.tensor_tensor(
+                    out=osb[b][:, 2 * n : 2 * n + 2, par, DN:DH].rearrange(pairs, two=2),
+                    in0=t[:, 0].rearrange(pairs, two=2),
+                    in1=t[:, 1].rearrange(pairs, two=2)[:, :, :, ::-1],
+                    op=ADD,
+                )
 
         def store(b, n):
             nc.sync.dma_start(
@@ -363,265 +349,293 @@ def tile_multiheadlatentattention_pa_w8_kernel(
                 in_=gain_ps[n][:].rearrange(by_word, u=2, e=2),
             )
 
+        warm_ps = bank(7, [P, P], F32, "warm_ps")
+        for k in range(24):
+            nc.tensor.matmul(warm_ps[:], ones[:], ones[:], start=True, stop=True)
         gain_mm(0, 0)
         cast_v(0, 0, 1024)
         cast_s(0, 1024, 2048)
         gain_mm(1, 1)
         gain_mm(2, 2)
-        cast_v(1, 0, 1024)
+        cast_v(1, 1024, 2048)
         turn_x(0, 0, 3)
-        gain_copy(0)
-        turn_x(0, 1, 4)
-        scale_x(0, 0)
-        scale_x(0, 1)
-        cast_s(1, 1024, 2048)
-        turn_x(1, 0, 5)
-        scale_x(0, 2)
-        scale_x(0, 3)
-        plane_x(1, 0)
-        plane_x(1, 1)
-        turn_x(1, 1, 6)
-        quant_x(0, 0, 2)
         nc.scalar.activation(out=warm[:], in_=ones[:, 0:1], func=ACT.Sqrt)
-        quant_x(0, 2, 4)
-        weave_x(1, 0, 2)
+        turn_x(0, 1, 4)
+        scale_x(0, 1)
+        turn_x(1, 1, 5)
+        scale_x(0, 2)
+        quant_x(0, 1, 2)
+        cast_s(1, 0, 1024)
+        scale_x(0, 0)
+        scale_x(0, 3)
+        gain_copy(2)
+        turn_x(1, 0, 6)
+        quant_x(0, 0, 1)
+        quant_x(0, 2, 3)
+        quant_x(0, 3, 4)
+        gain_copy(0)
         scale_x(1, 2)
         scale_x(1, 3)
-        mm_a(0, 0, 7)
-        gain_copy(2)
-        mm_a(0, 1, 0)
-        quant_x(1, 0, 4)
-        square(0, 0)
+        mm_a(0, 0, 7, (0,))
+        mm_a(0, 0, 0, (1,))
         gain_copy(1)
-        mm_a(1, 0, 3)
-        square(0, 1)
-        cast_v(2, 0, 1024)
+        mm_a(0, 0, 0, (2,))
+        mm_a(0, 0, 0, (3,))
+        scale_x(1, 0)
+        scale_x(1, 1)
+        mm_a(0, 1, 3)
         cast_s(2, 1024, 2048)
-        mm_a(0, 2, 4)
-        cast_v(3, 0, 1024)
-        square(1, 0)
+        cast_v(2, 0, 1024)
+        square(0, 0)
+        turn_x(2, 1, 4)
+        quant_x(1, 0, 4)
+        square(0, 1)
+        turn_x(2, 0, 2)
+        scale_x(2, 2)
+        scale_x(2, 3)
+        mm_a(0, 2, 0)
+        cast_s(3, 0, 1024)
         cast_v(3, 1024, 2048)
-        turn_x(2, 0, 5)
-        turn_x(2, 1, 6)
+        mm_a(1, 0, 1)
         square(0, 2)
         scale_x(2, 0)
         scale_x(2, 1)
-        mm_a(1, 2, 2)
         rms_a(0)
-        scale_x(2, 2)
-        scale_x(2, 3)
-        mm_a(1, 1, 1)
-        square(1, 2)
+        turn_x(3, 1, 5)
+        square(1, 0)
         rms_b(0)
-        quant_x(2, 0, 4)
-        norm_s(0, 2)
-        turn_x(3, 0, 5)
-        turn_x(3, 1, 6)
-        norm(0, 1)
-        square(1, 1)
-        norm_g(0, 2)
-        mm_a(2, 1, 4)
+        mm_a(1, 1, 6)
         scale_x(3, 2)
         scale_x(3, 3)
-        plane_x(3, 0)
-        plane_x(3, 1)
-        mm_a(2, 2, 0)
+        norm_s(0, 1)
+        mm_a(1, 2, 4)
+        norm_g(0, 1)
+        norm(0, 2)
+        square(1, 1)
         norm(0, 0)
+        turn_h(0, 1, 2)
+        square(1, 2)
+        turn_x(3, 0, 3)
+        quant_x(2, 0, 4)
+        turn_h(0, 0, 5)
+        copy_h(0, 1)
+        scale_x(3, 0)
+        scale_x(3, 1)
         rms_a(1)
-        weave_x(3, 0, 2)
+        mm_a(2, 2, 0)
+        copy_h(0, 0, nc.vector)
+        mm_a(2, 1, 7)
+        square(2, 2)
+        quant_x(3, 0, 4)
+        quant_h(0, 0)
+        mm_a(2, 0, 2)
+        quant_h(0, 1)
         square(2, 1)
-        mm_a(2, 0, 6)
         rms_b(1)
         norm(1, 1)
-        square(2, 2)
-        norm(1, 0)
-        turn_h(0, 1, 5)
-        square(2, 0)
-        turn_h(0, 0, 7)
-        quant_x(3, 0, 4)
-        turn_h(1, 0, 1)
-        copy_h(0, 1)
-        copy_h(0, 0, nc.vector)
-        rms_a(2)
         mm_a(3, 0, 3)
-        copy_h(1, 0)
-        quant_h(0, 1)
-        rms_b(2)
-        quant_h(0, 0)
-        norm_s(2, 1)
-        norm(2, 0)
-        mm_b(0, 1, 5)
-        norm_s(2, 2)
-        quant_h(1, 0)
-        mm_a(3, 2, 7)
+        square(2, 0)
         norm(1, 2)
-        norm_g(2, 1)
+        norm(1, 0)
+        rms_a(2)
+        mm_b(0, 3, 5)
         square(3, 0)
-        rope_mul(0, 1)
-        mm_b(0, 4, 1)
-        norm_g(2, 2)
-        square(3, 2)
-        mm_b(0, 2, 4)
-        nope(0, 1)
-        rope_mul(0, 4)
-        mm_a(3, 1, 6)
-        rope_add(0, 1, nc.gpsimd)
-        rope_mul(0, 2)
-        nope(0, 4)
-        rope_add(0, 4, nc.gpsimd)
-        nope(0, 2)
-        turn_h(2, 1, 0)
-        square(3, 1)
-        turn_h(1, 1, 2)
-        rope_add(0, 2, nc.gpsimd)
-        mm_b(0, 0, 5)
-        copy_h(1, 1, nc.vector)
-        copy_h(2, 1)
-        rms_a(3)
-        quant_h(1, 1)
-        mm_b(0, 7, 1)
-        quant_h(2, 1)
-        nope(0, 0)
-        rms_b(3)
-        rope_mul(0, 0)
-        mm_b(1, 6, 4)
-        norm_s(3, 2)
-        rope_mul(0, 7)
-        mm_b(1, 4, 2)
-        rope_add(0, 0, nc.gpsimd)
-        nope(1, 6)
-        norm(3, 0)
-        nope(0, 7)
-        mm_b(1, 1, 0)
-        rope_add(0, 7, nc.gpsimd)
-        nope(1, 4)
-        norm(3, 1)
-        mm_b(1, 3, 5)
-        norm_g(3, 2)
-        nope(1, 1)
-        rope_mul(1, 4)
-        mm_b(1, 0, 7)
-        nope(1, 3)
-        rope_mul(1, 1)
-        rope_add(1, 4, nc.gpsimd)
-        mm_b(1, 2, 1)
-        nope(1, 0)
-        rope_mul(1, 3)
-        rope_add(1, 1, nc.gpsimd)
-        turn_h(3, 1, 3)
-        store(0, 4)
-        rope_mul(1, 0)
-        nope(1, 2)
-        turn_h(3, 0, 6)
-        copy_h(3, 1)
-        turn_h(2, 0, 2)
-        rope_add(1, 3, nc.gpsimd)
-        rope_mul(1, 2)
-        copy_h(3, 0)
-        store(0, 1)
-        mm_b(0, 3, 0)
-        rope_add(1, 0, nc.vector)
-        copy_h(2, 0)
-        mm_b(0, 6, 5)
-        quant_h(3, 0)
-        store(0, 0)
+        rms_b(2)
+        mm_b(0, 6, 6)
+        norm(2, 1)
+        norm_s(2, 0)
+        mm_b(0, 7, 4)
+        norm(2, 2)
         nope(0, 3)
-        quant_h(3, 1)
-        quant_h(2, 0)
-        mm_b(1, 7, 7)
-        rope_mul(0, 3)
-        rope_add(1, 2, nc.gpsimd)
         nope(0, 6)
-        mm_b(3, 4, 3)
+        norm_g(2, 0)
+        mm_a(3, 2, 1)
         rope_mul(0, 6)
-        nope(1, 7)
+        nope(0, 7)
+        rope_mul(0, 7)
+        mm_b(0, 0, 7)
+        rope_add(0, 6, nc.vector)
+        square(3, 2)
+        rope_mul(0, 3)
+        mm_b(0, 4, 2)
+        swap(0, 7)
+        rope_mul(0, 0)
+        swap(0, 3)
+        mm_b(0, 2, 0)
+        rope_add(0, 7, nc.gpsimd)
+        nope(0, 4)
+        nope(0, 0)
+        rope_add(0, 0, nc.vector)
+        turn_h(1, 1, 6)
+        nope(0, 2)
+        turn_h(1, 0, 4)
         rope_add(0, 3, nc.gpsimd)
-        store(0, 2)
-        mm_b(2, 4, 1)
-        rope_mul(1, 7)
-        nope(3, 4)
-        rope_add(0, 6, nc.gpsimd)
-        store(0, 3)
-        rope_mul(3, 4)
-        mm_b(3, 7, 6)
-        nope(2, 4)
-        rope_add(1, 7, nc.gpsimd)
-        rope_mul(2, 4)
-        mm_b(2, 3, 2)
-        nope(3, 7)
-        rope_add(3, 4, nc.gpsimd)
-        rope_mul(1, 6)
-        store(0, 7)
-        mm_b(3, 0, 0)
-        nope(2, 3)
-        rope_add(2, 4, nc.gpsimd)
-        rope_mul(3, 7)
-        mm_b(3, 3, 5)
-        nope(3, 0)
-        rope_mul(2, 3)
-        rope_add(1, 6, nc.gpsimd)
-        mm_b(3, 6, 7)
-        store(1, 4)
-        nope(3, 3)
-        rope_mul(3, 0)
-        rope_add(3, 7, nc.gpsimd)
-        mm_b(2, 5, 3)
-        store(0, 6)
-        nope(3, 6)
-        rope_mul(3, 3)
-        rope_add(3, 0, nc.gpsimd)
-        mm_b(2, 1, 1)
-        rope_mul(3, 6)
-        nope(2, 5)
-        rope_add(2, 3, nc.gpsimd)
-        mm_b(2, 7, 4)
-        rope_mul(2, 5)
-        nope(2, 1)
-        rope_add(3, 3, nc.gpsimd)
-        mm_b(3, 1, 6)
-        rope_mul(2, 1)
-        nope(2, 7)
-        rope_add(2, 5, nc.gpsimd)
-        rope_mul(2, 7)
-        mm_b(2, 6, 2)
-        store(1, 3)
-        nope(3, 1)
-        rope_add(2, 1, nc.gpsimd)
-        rope_mul(3, 1)
-        mm_b(3, 5, 0)
-        nope(2, 6)
-        rope_add(2, 7, nc.vector)
-        mm_b(3, 2, 5)
-        nope(3, 5)
-        rope_add(3, 1, nc.vector)
-        store(1, 7)
-        rope_mul(3, 5)
-        rope_add(3, 6, nc.gpsimd)
-        mm_b(2, 2, 7)
-        store(1, 1)
-        nope(3, 2)
-        rope_mul(2, 6)
-        mm_b(2, 0, 3)
-        rope_add(3, 5, nc.gpsimd)
-        nope(2, 2)
-        rope_mul(3, 2)
-        mm_b(1, 5, 1)
-        rope_add(2, 6, nc.gpsimd)
-        nope(2, 0)
-        store(1, 5)
-        rope_mul(2, 2)
-        mm_b(0, 5, 4)
-        rope_add(3, 2, nc.gpsimd)
-        nope(1, 5)
-        rope_mul(2, 0)
-        store(1, 6)
-        nope(0, 5)
-        rope_add(2, 2, nc.vector)
+        rope_mul(0, 4)
+        copy_h(1, 1)
+        turn_h(2, 1, 5)
+        copy_h(1, 0)
+        mm_a(3, 1, 7)
+        rope_mul(0, 2)
+        copy_h(2, 1)
+        quant_h(1, 1)
+        swap(0, 4)
+        quant_h(1, 0)
+        mm_b(0, 5, 6)
+        swap(0, 2)
+        quant_h(2, 1)
+        rope_add(0, 4, nc.gpsimd)
+        square(3, 1)
+        mm_b(1, 2, 2)
         rope_mul(0, 5)
-        rope_add(2, 0, nc.gpsimd)
-        store(1, 2)
-        rope_mul(1, 5)
+        rope_add(0, 2, nc.gpsimd)
+        rms_a(3)
+        mm_b(1, 4, 4)
+        rope_mul(1, 2)
+        nope(0, 5)
+        swap(0, 5)
+        mm_b(1, 0, 0)
+        rms_b(3)
+        nope(1, 4)
         rope_add(0, 5, nc.gpsimd)
-        store(1, 0)
-        rope_add(1, 5, nc.vector)
+        swap(1, 2)
+        norm(3, 0)
+        mm_b(1, 3, 5)
+        norm_s(3, 2)
+        rope_add(1, 2, nc.gpsimd)
+        norm(3, 1)
+        mm_b(1, 1, 6)
+        nope(1, 0)
+        nope(1, 2)
+        norm_g(3, 2)
+        nope(1, 3)
+        rope_mul(1, 4)
+        store(0, 2)
+        mm_b(1, 6, 3)
+        nope(1, 1)
+        rope_mul(1, 3)
+        swap(1, 4)
+        turn_h(3, 0, 1)
+        nope(1, 6)
+        rope_mul(1, 1)
+        turn_h(2, 0, 2)
+        rope_add(1, 4, nc.gpsimd)
+        swap(1, 3)
+        turn_h(3, 1, 7)
+        copy_h(3, 0)
+        rope_mul(1, 0)
+        mm_b(1, 5, 4)
+        rope_add(1, 3, nc.gpsimd)
+        store(0, 4)
+        copy_h(3, 1)
+        rope_mul(1, 6)
+        mm_b(0, 1, 5)
+        copy_h(2, 0)
+        store(0, 3)
+        rope_add(1, 0, nc.vector)
+        nope(1, 5)
+        mm_b(1, 7, 6)
+        quant_h(3, 0)
+        swap(1, 6)
+        store(0, 0)
+        quant_h(2, 0)
+        nope(0, 1)
+        swap(1, 1)
+        quant_h(3, 1)
+        rope_mul(1, 5)
+        rope_add(1, 6, nc.gpsimd)
+        mm_b(2, 5, 1)
+        nope(1, 7)
+        rope_mul(1, 7)
+        rope_add(1, 1, nc.gpsimd)
+        mm_b(3, 0, 0)
+        swap(1, 5)
+        store(0, 6)
+        nope(2, 5)
+        rope_mul(0, 1)
+        mm_b(3, 4, 7)
+        rope_add(1, 5, nc.gpsimd)
+        swap(1, 7)
+        nope(3, 0)
+        rope_mul(2, 5)
+        swap(0, 1)
+        mm_b(3, 6, 3)
+        rope_add(1, 7, nc.gpsimd)
         store(0, 5)
+        nope(3, 4)
+        rope_mul(3, 0)
+        swap(2, 5)
+        mm_b(3, 7, 2)
+        rope_add(0, 1, nc.gpsimd)
+        nope(3, 6)
+        store(0, 7)
+        rope_mul(3, 4)
+        swap(3, 0)
+        mm_b(2, 4, 4)
+        rope_add(2, 5, nc.gpsimd)
+        rope_mul(3, 6)
+        nope(3, 7)
+        store(0, 1)
+        swap(3, 4)
+        mm_b(2, 0, 6)
+        rope_add(3, 0, nc.gpsimd)
+        rope_mul(3, 7)
+        nope(2, 4)
+        mm_b(2, 7, 5)
+        rope_mul(2, 4)
+        rope_add(3, 4, nc.gpsimd)
+        nope(2, 0)
+        mm_b(3, 3, 1)
+        rope_mul(2, 0)
+        swap(2, 4)
+        nope(2, 7)
+        rope_add(3, 6, nc.vector)
+        mm_b(2, 3, 0)
+        swap(2, 0)
+        rope_add(3, 7, nc.vector)
+        nope(3, 3)
+        rope_add(2, 4, nc.gpsimd)
+        rope_mul(2, 7)
+        mm_b(2, 6, 7)
+        nope(2, 3)
+        rope_mul(3, 3)
+        mm_b(3, 5, 3)
+        rope_add(2, 0, nc.gpsimd)
+        swap(2, 7)
+        store(1, 4)
+        nope(2, 6)
+        rope_mul(2, 3)
+        mm_b(2, 2, 2)
+        rope_add(2, 7, nc.gpsimd)
+        nope(3, 5)
+        store(1, 0)
+        rope_mul(2, 6)
+        swap(2, 3)
+        mm_b(3, 1, 4)
+        store(1, 7)
+        nope(2, 2)
+        rope_add(3, 3, nc.vector)
+        swap(2, 6)
+        mm_b(3, 2, 6)
+        rope_add(2, 3, nc.gpsimd)
+        rope_mul(3, 5)
+        nope(3, 1)
+        mm_b(2, 1, 5)
+        rope_mul(2, 2)
+        rope_add(2, 6, nc.gpsimd)
+        swap(3, 5)
+        store(1, 3)
+        nope(3, 2)
+        rope_mul(3, 1)
+        rope_add(3, 5, nc.gpsimd)
+        swap(2, 2)
+        store(1, 6)
+        nope(2, 1)
+        rope_mul(3, 2)
+        rope_add(2, 2, nc.gpsimd)
+        store(1, 5)
+        rope_mul(2, 1)
+        rope_add(3, 2, nc.vector)
+        rope_add(2, 1, nc.vector)
+        store(1, 2)
+        rope_add(3, 1, nc.vector)
+        store(1, 1)

@@ -66,7 +66,7 @@ def tile_multiheadlatentattention_pa_w8_kernel(
         kint = keep.tile([P, 2, 2, 64], I32, name="kint")
         frac = keep.tile([P, 2, 2, 64], F32, name="frac")
         tab = keep.tile([P, 2, 2, P], F32, name="tab")
-        warm = keep.tile([P, 1], F32, name="warm")
+        mhalf = keep.tile([P, 1], F32, name="mhalf")
         one32 = keep.tile([P, 1], F32, name="one32")
         osb = [keep.tile([P, H, 2, DH], F32, name="osb_%d" % (i,)) for i in range(2)]
 
@@ -80,11 +80,12 @@ def tile_multiheadlatentattention_pa_w8_kernel(
         nc.vector.memset(was[:].bitcast(I32), 0)
         nc.vector.memset(gz[:], 0.0)
         nc.vector.memset(one32[:], 1.0)
+        nc.vector.memset(mhalf[:], -0.5)
 
-        def load_x(i):
+        def load_x(i, lo=0, hi=D):
             b, par = divmod(i, 2)
             nc.sync.dma_start(
-                out=x8[i][:], in_=x_bytes[b].rearrange("(p two) k -> p two k", two=2)[:, par, :]
+                out=x8[i][:, lo:hi], in_=x_bytes[b].rearrange("(p two) k -> p two k", two=2)[:, par, lo:hi]
             )
 
         def load_scales(tile, dram, groups):
@@ -103,7 +104,8 @@ def tile_multiheadlatentattention_pa_w8_kernel(
 
         nc.scalar.dma_start(out=xs[:], in_=x_scale.rearrange("a b (g p t) -> p (a b g) t", p=P, t=4))
         nc.scalar.dma_start(out=gz[0:1, :], in_=q_a_norm_w.unsqueeze(0))
-        load_x(0)
+        load_x(0, 0, D // 2)
+        load_x(0, D // 2, D)
         load_scales(was, Wqa_scales, GA)
         load_x(1)
         load_w(wa[0], Wqa_words, 0)
@@ -174,6 +176,43 @@ def tile_multiheadlatentattention_pa_w8_kernel(
                 op=MUL,
             )
 
+        planes = {}
+
+        def plane_x(i, g):
+            pt = trx[i, g // 2]
+            xp = work.tile([P, 4, P], BF16, name="xp", bufs=4)
+            planes[i, g] = xp
+            for t in range(4):
+                u, e = divmod(t, 2)
+                nc.scalar.activation(
+                    out=xp[:, t, :],
+                    in_=pt[:, g % 2, u, :].bitcast(BF16)[:, e::2],
+                    func=ACT.Copy,
+                    scale=xs[:, g, t : t + 1],
+                )
+
+        def spread_x(i, g):
+            pt = trx[i, g // 2]
+            dst = xg[i][:, 512 * g : 512 * (g + 1)].rearrange("p (r t) -> p r t", t=4)
+            for t in range(4):
+                u, e = divmod(t, 2)
+                nc.scalar.activation(
+                    out=dst[:, :, t],
+                    in_=pt[:, g % 2, u, :].bitcast(BF16)[:, e::2],
+                    func=ACT.Copy,
+                    scale=xs[:, g, t : t + 1],
+                )
+
+        def weave_x(i, g):
+            nc.gpsimd.tensor_scalar(
+                out=xg[i][:, 512 * g : 512 * (g + 1)].rearrange("p (r t) -> p r t", t=4),
+                in0=planes[i, g][:].rearrange("p t r -> p r t"),
+                scalar1=1.0,
+                scalar2=0.0,
+                op0=MUL,
+                op1=ADD,
+            )
+
         def quant_x(i, g0, g1):
             nc.vector.quantize_mx(
                 out=xq[i][:, P * g0 : P * g1].bitcast(FP8X4),
@@ -203,10 +242,10 @@ def tile_multiheadlatentattention_pa_w8_kernel(
 
         def rms_a(i):
             nc.scalar.activation(out=rms[i][:, 4:7], in_=ssq[i][:, 0:3], func=ACT.Copy, accum_out=rms[i][:, 0:1])
-            nc.scalar.activation(out=rms[i][:, 2:3], in_=rms[i][:, 0:1], func=ACT.Sqrt, scale=1.0 / RQ, bias=EPS)
 
         def rms_b(i):
-            nc.vector.reciprocal(out=rms[i][:, 3:4], in_=rms[i][:, 2:3])
+            nc.gpsimd.tensor_scalar(out=rms[i][:, 2:3], in0=rms[i][:, 0:1], scalar1=1.0 / RQ, scalar2=EPS, op0=MUL, op1=ADD)
+            nc.gpsimd.tensor_tensor(out=rms[i][:, 3:4], in0=rms[i][:, 2:3], in1=mhalf[:], op=mybir.AluOpType.pow)
 
         by_word = "p (q u e) -> p u q e"
 
@@ -217,7 +256,7 @@ def tile_multiheadlatentattention_pa_w8_kernel(
                     out=hb[i][:, cols].rearrange("p (q e) -> p q e", e=2),
                     in0=acc[i, n][:].rearrange(by_word, u=2, e=2)[:, u],
                     scalar=rms[i][:, 3:4],
-                    in1=gbc[:, cols].rearrange("p (q e) -> p q e", e=2),
+                    in1=gbc[:, 512 * n : 512 * (n + 1)].rearrange(by_word, u=2, e=2)[:, u],
                     op0=MUL,
                     op1=MUL,
                 )
@@ -235,7 +274,14 @@ def tile_multiheadlatentattention_pa_w8_kernel(
             )
 
         def norm_g(i, n):
-            nc.gpsimd.tensor_tensor(out=hb[i][:, 512 * n : 512 * (n + 1)], in0=hs[i, n][:], in1=gbc[:, 512 * n : 512 * (n + 1)], op=MUL)
+            cols = slice(512 * n, 512 * (n + 1))
+            sorted_words = "p (u q e) -> p u q e"
+            nc.gpsimd.tensor_tensor(
+                out=hb[i][:, cols].rearrange(sorted_words, u=2, e=2),
+                in0=hs[i, n][:].rearrange(sorted_words, u=2, e=2),
+                in1=gbc[:, cols].rearrange(by_word, u=2, e=2),
+                op=MUL,
+            )
 
         trh = {}
 
@@ -339,303 +385,283 @@ def tile_multiheadlatentattention_pa_w8_kernel(
         gain_ps = {}
 
         def gain_mm(n, b):
-            gp = bank(b, [P, 512], F32, "gain%d" % (n,))
+            gp = bank(b, [P, 512], BF16, "gain%d" % (n,))
             gain_ps[n] = gp
             nc.tensor.matmul(gp[:], ones[:], gz[:, 512 * n : 512 * (n + 1)], start=True, stop=True)
 
-        def gain_copy(n):
-            nc.scalar.copy(
-                out=gbc[:, 512 * n : 512 * (n + 1)].rearrange("p (u q e) -> p u q e", u=2, e=2),
-                in_=gain_ps[n][:].rearrange(by_word, u=2, e=2),
-            )
+        def gain_copy(n, copy):
+            copy(out=gbc[:, 512 * n : 512 * (n + 1)], in_=gain_ps[n][:])
 
         warm_ps = bank(7, [P, P], F32, "warm_ps")
         for k in range(24):
             nc.tensor.matmul(warm_ps[:], ones[:], ones[:], start=True, stop=True)
-        gain_mm(0, 0)
         cast_v(0, 0, 1024)
-        cast_s(0, 1024, 2048)
-        gain_mm(1, 1)
-        gain_mm(2, 2)
+        gain_mm(1, 0)
+        gain_mm(0, 1)
+        cast_v(0, 1024, 2048)
+        gain_copy(1, nc.scalar.copy)
+        turn_x(0, 0, 2)
+        gain_copy(0, nc.scalar.copy)
         cast_v(1, 1024, 2048)
-        turn_x(0, 0, 3)
-        nc.scalar.activation(out=warm[:], in_=ones[:, 0:1], func=ACT.Sqrt)
-        turn_x(0, 1, 4)
-        scale_x(0, 1)
-        turn_x(1, 1, 5)
-        scale_x(0, 2)
-        quant_x(0, 1, 2)
+        gain_mm(2, 3)
         cast_s(1, 0, 1024)
+        turn_x(0, 1, 4)
         scale_x(0, 0)
-        scale_x(0, 3)
-        gain_copy(2)
+        turn_x(1, 1, 5)
+        scale_x(0, 1)
+        plane_x(0, 3)
         turn_x(1, 0, 6)
         quant_x(0, 0, 1)
-        quant_x(0, 2, 3)
-        quant_x(0, 3, 4)
-        gain_copy(0)
-        scale_x(1, 2)
-        scale_x(1, 3)
+        spread_x(1, 2)
+        quant_x(0, 1, 2)
+        scale_x(0, 2)
+        weave_x(0, 3)
         mm_a(0, 0, 7, (0,))
         mm_a(0, 0, 0, (1,))
-        gain_copy(1)
-        mm_a(0, 0, 0, (2,))
-        mm_a(0, 0, 0, (3,))
-        scale_x(1, 0)
         scale_x(1, 1)
-        mm_a(0, 1, 3)
-        cast_s(2, 1024, 2048)
+        quant_x(0, 3, 4)
+        quant_x(0, 2, 3)
+        scale_x(1, 0)
+        gain_copy(2, nc.scalar.copy)
+        mm_a(0, 0, 0, (2,))
+        spread_x(1, 3)
+        mm_a(0, 0, 0, (3,))
+        mm_a(0, 1, 0)
+        quant_x(1, 0, 2)
+        cast_v(2, 1024, 2048)
         cast_v(2, 0, 1024)
-        square(0, 0)
-        turn_x(2, 1, 4)
-        quant_x(1, 0, 4)
         square(0, 1)
+        turn_x(2, 1, 1)
+        quant_x(1, 2, 4)
+        square(0, 0)
         turn_x(2, 0, 2)
         scale_x(2, 2)
+        mm_a(1, 1, 4)
+        plane_x(2, 1)
         scale_x(2, 3)
-        mm_a(0, 2, 0)
-        cast_s(3, 0, 1024)
         cast_v(3, 1024, 2048)
-        mm_a(1, 0, 1)
-        square(0, 2)
-        scale_x(2, 0)
-        scale_x(2, 1)
-        rms_a(0)
-        turn_x(3, 1, 5)
-        square(1, 0)
-        rms_b(0)
-        mm_a(1, 1, 6)
-        scale_x(3, 2)
-        scale_x(3, 3)
-        norm_s(0, 1)
-        mm_a(1, 2, 4)
-        norm_g(0, 1)
-        norm(0, 2)
+        mm_a(0, 2, 3)
         square(1, 1)
-        norm(0, 0)
-        turn_h(0, 1, 2)
+        quant_x(2, 2, 4)
+        scale_x(2, 0)
+        weave_x(2, 1)
+        mm_a(1, 2, 6)
+        square(0, 2)
+        cast_v(3, 0, 1024)
+        rms_a(0)
+        mm_a(1, 0, 5)
+        quant_x(2, 0, 2)
         square(1, 2)
-        turn_x(3, 0, 3)
-        quant_x(2, 0, 4)
-        turn_h(0, 0, 5)
-        copy_h(0, 1)
-        scale_x(3, 0)
-        scale_x(3, 1)
+        rms_b(0)
+        norm(0, 1)
+        mm_a(2, 0, 1)
+        square(1, 0)
+        norm(0, 2)
         rms_a(1)
-        mm_a(2, 2, 0)
-        copy_h(0, 0, nc.vector)
-        mm_a(2, 1, 7)
-        square(2, 2)
-        quant_x(3, 0, 4)
-        quant_h(0, 0)
-        mm_a(2, 0, 2)
-        quant_h(0, 1)
-        square(2, 1)
+        mm_a(2, 1, 2)
+        norm(0, 0)
         rms_b(1)
-        norm(1, 1)
-        mm_a(3, 0, 3)
         square(2, 0)
-        norm(1, 2)
         norm(1, 0)
-        rms_a(2)
-        mm_b(0, 3, 5)
-        square(3, 0)
-        rms_b(2)
-        mm_b(0, 6, 6)
-        norm(2, 1)
-        norm_s(2, 0)
-        mm_b(0, 7, 4)
-        norm(2, 2)
+        norm_s(1, 2)
+        turn_h(0, 1, 0)
+        turn_h(0, 0, 3)
+        square(2, 1)
+        norm(1, 1)
+        norm_g(1, 2)
+        turn_x(3, 0, 7)
+        turn_x(3, 1, 6)
+        copy_h(0, 0)
+        copy_h(0, 1, nc.vector)
+        mm_a(2, 2, 5)
+        scale_x(3, 3)
+        plane_x(3, 0)
+        quant_h(0, 0)
+        spread_x(3, 1)
+        quant_h(0, 1)
+        weave_x(3, 0)
+        scale_x(3, 2)
+        turn_h(1, 1, 4)
+        turn_h(1, 0, 0)
+        copy_h(1, 1, nc.vector)
+        mm_b(0, 2, 3)
+        quant_x(3, 2, 4)
+        quant_h(1, 1)
+        mm_b(0, 4, 6)
+        square(2, 2)
+        rope_mul(0, 2)
+        mm_b(0, 3, 4)
+        copy_h(1, 0)
+        quant_x(3, 0, 2)
+        rope_mul(0, 4)
+        mm_b(0, 7, 7)
+        nope(0, 2)
         nope(0, 3)
-        nope(0, 6)
-        norm_g(2, 0)
-        mm_a(3, 2, 1)
-        rope_mul(0, 6)
+        quant_h(1, 0)
+        rms_a(2)
+        nope(0, 4)
+        mm_a(3, 2, 0)
+        rope_mul(0, 3)
+        rope_add(0, 4, nc.gpsimd)
         nope(0, 7)
         rope_mul(0, 7)
-        mm_b(0, 0, 7)
-        rope_add(0, 6, nc.vector)
+        rms_b(2)
+        mm_b(1, 4, 3)
+        rope_add(0, 3, nc.vector)
         square(3, 2)
-        rope_mul(0, 3)
-        mm_b(0, 4, 2)
-        swap(0, 7)
-        rope_mul(0, 0)
-        swap(0, 3)
-        mm_b(0, 2, 0)
+        norm(2, 0)
         rope_add(0, 7, nc.gpsimd)
-        nope(0, 4)
-        nope(0, 0)
-        rope_add(0, 0, nc.vector)
-        turn_h(1, 1, 6)
-        nope(0, 2)
-        turn_h(1, 0, 4)
-        rope_add(0, 3, nc.gpsimd)
-        rope_mul(0, 4)
-        copy_h(1, 1)
-        turn_h(2, 1, 5)
-        copy_h(1, 0)
-        mm_a(3, 1, 7)
-        rope_mul(0, 2)
-        copy_h(2, 1)
-        quant_h(1, 1)
-        swap(0, 4)
-        quant_h(1, 0)
-        mm_b(0, 5, 6)
-        swap(0, 2)
-        quant_h(2, 1)
-        rope_add(0, 4, nc.gpsimd)
-        square(3, 1)
-        mm_b(1, 2, 2)
-        rope_mul(0, 5)
-        rope_add(0, 2, nc.gpsimd)
-        rms_a(3)
-        mm_b(1, 4, 4)
-        rope_mul(1, 2)
-        nope(0, 5)
-        swap(0, 5)
-        mm_b(1, 0, 0)
-        rms_b(3)
+        mm_b(1, 2, 6)
+        norm_s(2, 1)
+        norm(2, 2)
+        mm_b(1, 7, 4)
         nope(1, 4)
-        rope_add(0, 5, nc.gpsimd)
-        swap(1, 2)
-        norm(3, 0)
-        mm_b(1, 3, 5)
-        norm_s(3, 2)
-        rope_add(1, 2, nc.gpsimd)
-        norm(3, 1)
-        mm_b(1, 1, 6)
-        nope(1, 0)
         nope(1, 2)
-        norm_g(3, 2)
-        nope(1, 3)
+        norm_g(2, 1)
         rope_mul(1, 4)
-        store(0, 2)
-        mm_b(1, 6, 3)
-        nope(1, 1)
-        rope_mul(1, 3)
-        swap(1, 4)
-        turn_h(3, 0, 1)
-        nope(1, 6)
-        rope_mul(1, 1)
-        turn_h(2, 0, 2)
-        rope_add(1, 4, nc.gpsimd)
-        swap(1, 3)
-        turn_h(3, 1, 7)
-        copy_h(3, 0)
-        rope_mul(1, 0)
-        mm_b(1, 5, 4)
-        rope_add(1, 3, nc.gpsimd)
-        store(0, 4)
-        copy_h(3, 1)
-        rope_mul(1, 6)
-        mm_b(0, 1, 5)
-        copy_h(2, 0)
-        store(0, 3)
-        rope_add(1, 0, nc.vector)
-        nope(1, 5)
-        mm_b(1, 7, 6)
-        quant_h(3, 0)
-        swap(1, 6)
-        store(0, 0)
-        quant_h(2, 0)
-        nope(0, 1)
-        swap(1, 1)
-        quant_h(3, 1)
-        rope_mul(1, 5)
-        rope_add(1, 6, nc.gpsimd)
-        mm_b(2, 5, 1)
+        mm_b(1, 5, 7)
         nope(1, 7)
+        rope_mul(1, 2)
+        mm_b(1, 0, 1)
+        rope_add(1, 4, nc.gpsimd)
+        nope(1, 5)
         rope_mul(1, 7)
-        rope_add(1, 1, nc.gpsimd)
-        mm_b(3, 0, 0)
-        swap(1, 5)
-        store(0, 6)
-        nope(2, 5)
-        rope_mul(0, 1)
-        mm_b(3, 4, 7)
+        mm_a(3, 1, 2)
+        nope(1, 0)
+        rope_add(1, 2, nc.gpsimd)
+        rope_mul(1, 5)
+        store(0, 4)
+        rope_add(1, 7, nc.vector)
+        mm_a(3, 0, 5)
+        rope_mul(1, 0)
         rope_add(1, 5, nc.gpsimd)
-        swap(1, 7)
-        nope(3, 0)
-        rope_mul(2, 5)
-        swap(0, 1)
-        mm_b(3, 6, 3)
-        rope_add(1, 7, nc.gpsimd)
-        store(0, 5)
-        nope(3, 4)
-        rope_mul(3, 0)
-        swap(2, 5)
-        mm_b(3, 7, 2)
-        rope_add(0, 1, nc.gpsimd)
-        nope(3, 6)
+        square(3, 1)
         store(0, 7)
-        rope_mul(3, 4)
-        swap(3, 0)
-        mm_b(2, 4, 4)
-        rope_add(2, 5, nc.gpsimd)
-        rope_mul(3, 6)
-        nope(3, 7)
-        store(0, 1)
-        swap(3, 4)
-        mm_b(2, 0, 6)
-        rope_add(3, 0, nc.gpsimd)
-        rope_mul(3, 7)
-        nope(2, 4)
-        mm_b(2, 7, 5)
-        rope_mul(2, 4)
-        rope_add(3, 4, nc.gpsimd)
-        nope(2, 0)
-        mm_b(3, 3, 1)
-        rope_mul(2, 0)
-        swap(2, 4)
-        nope(2, 7)
-        rope_add(3, 6, nc.vector)
-        mm_b(2, 3, 0)
-        swap(2, 0)
-        rope_add(3, 7, nc.vector)
-        nope(3, 3)
-        rope_add(2, 4, nc.gpsimd)
-        rope_mul(2, 7)
-        mm_b(2, 6, 7)
-        nope(2, 3)
-        rope_mul(3, 3)
-        mm_b(3, 5, 3)
-        rope_add(2, 0, nc.gpsimd)
-        swap(2, 7)
-        store(1, 4)
-        nope(2, 6)
-        rope_mul(2, 3)
-        mm_b(2, 2, 2)
-        rope_add(2, 7, nc.gpsimd)
-        nope(3, 5)
-        store(1, 0)
-        rope_mul(2, 6)
-        swap(2, 3)
-        mm_b(3, 1, 4)
-        store(1, 7)
-        nope(2, 2)
-        rope_add(3, 3, nc.vector)
-        swap(2, 6)
-        mm_b(3, 2, 6)
-        rope_add(2, 3, nc.gpsimd)
-        rope_mul(3, 5)
-        nope(3, 1)
-        mm_b(2, 1, 5)
-        rope_mul(2, 2)
-        rope_add(2, 6, nc.gpsimd)
-        swap(3, 5)
-        store(1, 3)
-        nope(3, 2)
-        rope_mul(3, 1)
-        rope_add(3, 5, nc.gpsimd)
-        swap(2, 2)
-        store(1, 6)
+        rope_add(0, 2, nc.vector)
+        mm_b(1, 6, 3)
+        rope_add(1, 0, nc.gpsimd)
+        square(3, 0)
+        store(0, 2)
+        mm_b(1, 3, 6)
+        rope_mul(1, 6)
+        rms_a(3)
+        mm_b(1, 1, 4)
+        rms_b(3)
+        rope_mul(1, 3)
+        nope(1, 6)
+        rope_add(1, 6, nc.gpsimd)
+        mm_b(0, 5, 7)
+        norm_s(3, 1)
+        norm(3, 0)
+        rope_add(1, 3, nc.gpsimd)
+        nope(1, 1)
+        mm_b(0, 1, 1)
+        nope(1, 3)
+        norm(3, 2)
+        nope(0, 5)
+        norm_g(3, 1)
+        store(0, 3)
+        turn_h(2, 0, 3)
+        rope_mul(1, 1)
+        nope(0, 1)
+        turn_h(3, 1, 2)
+        turn_h(2, 1, 5)
+        copy_h(2, 0)
+        rope_mul(0, 5)
+        mm_b(0, 0, 6)
+        rope_add(1, 1, nc.gpsimd)
+        copy_h(3, 1)
+        rope_mul(0, 1)
+        copy_h(2, 1)
+        turn_h(3, 0, 0)
+        nope(0, 0)
+        quant_h(2, 0)
+        mm_b(0, 6, 4)
+        copy_h(3, 0)
+        quant_h(2, 1)
+        rope_add(0, 5, nc.vector)
+        quant_h(3, 1)
+        mm_b(2, 1, 3)
+        rope_mul(0, 0)
+        rope_add(0, 1, nc.gpsimd)
+        store(0, 5)
+        nope(0, 6)
+        mm_b(2, 2, 7)
+        quant_h(3, 0)
         nope(2, 1)
-        rope_mul(3, 2)
-        rope_add(2, 2, nc.gpsimd)
-        store(1, 5)
+        store(0, 1)
+        rope_add(0, 0, nc.gpsimd)
+        rope_mul(0, 6)
+        mm_b(2, 6, 2)
+        nope(2, 2)
         rope_mul(2, 1)
-        rope_add(3, 2, nc.vector)
-        rope_add(2, 1, nc.vector)
-        store(1, 2)
-        rope_add(3, 1, nc.vector)
+        rope_add(0, 6, nc.gpsimd)
+        mm_b(3, 6, 5)
+        store(0, 0)
+        nope(2, 6)
+        rope_mul(2, 2)
+        rope_add(2, 1, nc.gpsimd)
+        mm_b(3, 3, 1)
+        store(0, 6)
+        nope(3, 6)
+        rope_mul(2, 6)
+        mm_b(3, 1, 0)
+        rope_add(2, 2, nc.gpsimd)
+        rope_mul(3, 6)
+        nope(3, 3)
+        mm_b(2, 3, 6)
+        rope_add(2, 6, nc.gpsimd)
+        rope_mul(3, 3)
+        nope(3, 1)
+        mm_b(2, 4, 4)
+        rope_add(3, 6, nc.gpsimd)
+        rope_mul(3, 1)
+        nope(2, 3)
+        mm_b(3, 2, 3)
+        rope_mul(2, 3)
+        rope_add(3, 1, nc.gpsimd)
+        nope(2, 4)
+        store(1, 6)
+        rope_mul(2, 4)
+        mm_b(3, 4, 7)
+        nope(3, 2)
+        rope_add(2, 3, nc.gpsimd)
         store(1, 1)
+        rope_mul(3, 2)
+        mm_b(2, 5, 2)
+        nope(3, 4)
+        rope_add(3, 3, nc.vector)
+        mm_b(3, 5, 5)
+        rope_add(2, 4, nc.vector)
+        nope(2, 5)
+        store(1, 3)
+        rope_add(3, 2, nc.gpsimd)
+        rope_mul(3, 4)
+        mm_b(2, 0, 1)
+        nope(3, 5)
+        rope_mul(2, 5)
+        rope_add(3, 4, nc.gpsimd)
+        mm_b(3, 0, 0)
+        store(1, 2)
+        nope(2, 0)
+        rope_mul(3, 5)
+        mm_b(3, 7, 6)
+        rope_add(2, 5, nc.gpsimd)
+        store(1, 4)
+        nope(3, 0)
+        rope_mul(2, 0)
+        mm_b(2, 7, 4)
+        rope_add(3, 5, nc.gpsimd)
+        nope(3, 7)
+        rope_mul(3, 0)
+        rope_add(2, 0, nc.gpsimd)
+        rope_mul(3, 7)
+        nope(2, 7)
+        store(1, 5)
+        rope_add(3, 0, nc.vector)
+        rope_mul(2, 7)
+        rope_add(3, 7, nc.gpsimd)
+        store(1, 0)
+        rope_add(2, 7, nc.vector)
+        store_one(3, 7)
+        store_one(2, 7)

import math
from contextlib import ExitStack

import concourse.mybir as mybir
from concourse.masks import make_identity

B, S, D, H, DN, DR, RQ = 2, 256, 2048, 16, 64, 128, 1536
DH = DN + DR
NQ = H * DH
THETA = 10000.0
EPS = 1e-6
P = 128
FLOPS = 2 * B * S * D * RQ + 2 * B * S * RQ * NQ

F32 = mybir.dt.float32
BF16 = mybir.dt.bfloat16
I32 = mybir.dt.int32
U32 = mybir.dt.uint32
U8 = mybir.dt.uint8
FP8 = mybir.dt.float8_e4m3fn
FP8X4 = mybir.dt.float8_e4m3fn_x4
ADD = mybir.AluOpType.add
SUB = mybir.AluOpType.subtract
MUL = mybir.AluOpType.mult
ACT = mybir.ActivationFunctionType
AX = mybir.AxisListType

GA = D // 512
GB = RQ // 512
NB = H // 2
WB = 2 * DH


def tile_multiheadlatentattention_pa_w8_kernel(
    tc, x_bytes, x_scale, Wqa_words, Wqa_scales, q_a_norm_w, Wqb_words, Wqb_scales, out
):
    nc = tc.nc
    with ExitStack() as ctx:
        keep = ctx.enter_context(tc.tile_pool(name="keep", bufs=1))
        work = ctx.enter_context(tc.tile_pool(name="work", bufs=4))
        psum = ctx.enter_context(tc.psum_pool(name="psum", bufs=1))
        ctx.enter_context(tc.manual_schedule())

        x8 = [keep.tile([P, D], U8, name="x8_%d" % (i,)) for i in range(4)]
        xb = [keep.tile([P, D], BF16, name="xb_%d" % (i,), align_bytes=64) for i in range(4)]
        xg = [keep.tile([P, D], BF16, name="xg_%d" % (i,), align_bytes=64) for i in range(4)]
        xq = [keep.tile([P, GA * P], U32, name="xq_%d" % (i,), align_bytes=64) for i in range(4)]
        xqs = [keep.tile([P, GA * P], U8, name="xqs_%d" % (i,), align_bytes=64) for i in range(4)]
        hb = [keep.tile([P, RQ], BF16, name="hb_%d" % (i,), align_bytes=64) for i in range(4)]
        hg = [keep.tile([P, RQ], BF16, name="hg_%d" % (i,), align_bytes=64) for i in range(4)]
        hq = [keep.tile([P, GB * P], U32, name="hq_%d" % (i,), align_bytes=64) for i in range(4)]
        hqs = [keep.tile([P, GB * P], U8, name="hqs_%d" % (i,), align_bytes=64) for i in range(4)]
        ssq = [keep.tile([P, 8], F32, name="ssq_%d" % (i,)) for i in range(4)]
        rms = [keep.tile([P, 8], F32, name="rms_%d" % (i,)) for i in range(4)]
        wa = [keep.tile([P, GA, 512], U32, name="wa_%d" % (i,), align_bytes=64) for i in range(GB)]
        wb = [keep.tile([P, GB, 2 * WB], U32, name="wb_%d" % (i,), align_bytes=64) for i in range(NB // 2)]
        was = keep.tile([P, RQ], U8, name="was", align_bytes=64)
        wbs = keep.tile([P, NQ], U8, name="wbs", align_bytes=64)
        xs = keep.tile([P, GA, 4], F32, name="xs")
        gz = keep.tile([P, RQ], BF16, name="gz", align_bytes=64)
        gbc = keep.tile([P, RQ], BF16, name="gbc", align_bytes=64)
        ones = keep.tile([P, P], BF16, name="ones", align_bytes=64)
        ident = keep.tile([P, P], F32, name="ident", align_bytes=64)
        pos = keep.tile([P, 2], I32, name="pos")
        turns = keep.tile([P, 2, 64], F32, name="turns")
        kint = keep.tile([P, 2, 2, 64], I32, name="kint")
        frac = keep.tile([P, 2, 2, 64], F32, name="frac")
        tab = keep.tile([P, 2, 2, P], F32, name="tab")
        mhalf = keep.tile([P, 1], F32, name="mhalf")
        one32 = keep.tile([P, 1], F32, name="one32")
        osb = [keep.tile([P, H, 2, DH], F32, name="osb_%d" % (i,)) for i in range(2)]

        def bank(i, shape, dtype, name):
            return psum.tile(shape, dtype, name=name, tag="bank%d" % (i,), bufs=1)

        nc.gpsimd.iota(pos[:], pattern=[[1, 2]], base=0, channel_multiplier=2)
        make_identity(nc, ident[:])
        nc.gpsimd.memset(wbs[:].bitcast(I32), 0)
        nc.vector.memset(ones[:], 1.0)
        nc.vector.memset(was[:].bitcast(I32), 0)
        nc.vector.memset(gz[:], 0.0)
        nc.vector.memset(one32[:], 1.0)
        nc.vector.memset(mhalf[:], -0.5)

        def load_x(i, lo=0, hi=D):
            b, par = divmod(i, 2)
            nc.sync.dma_start(
                out=x8[i][:, lo:hi], in_=x_bytes[b].rearrange("(p two) k -> p two k", two=2)[:, par, lo:hi]
            )

        def load_scales(tile, dram, groups):
            for q in range(4):
                nc.sync.dma_start(
                    out=tile[32 * q : 32 * q + 4 * groups, :].bitcast(I32),
                    in_=dram[:, 4 * q : 4 * q + 4, :].bitcast(I32),
                )

        def load_w(tile, dram, n):
            w = tile.shape[2]
            nc.sync.dma_start(
                out=tile[:].bitcast(I32),
                in_=dram.rearrange("g p n t -> p g (n t)")[:, :, 4 * w * n : 4 * w * (n + 1)].bitcast(I32),
            )

        nc.scalar.dma_start(out=xs[:], in_=x_scale.rearrange("a b (g p t) -> p (a b g) t", p=P, t=4))
        nc.scalar.dma_start(out=gz[0:1, :], in_=q_a_norm_w.unsqueeze(0))
        load_x(0, 0, D // 2)
        load_x(0, D // 2, D)
        load_scales(was, Wqa_scales, GA)
        load_x(1)
        load_w(wa[0], Wqa_words, 0)
        load_w(wa[1], Wqa_words, 1)
        load_x(2)
        load_w(wa[2], Wqa_words, 2)
        load_x(3)
        load_scales(wbs, Wqb_scales, GB)
        load_w(wb[0], Wqb_words, 0)
        load_w(wb[1], Wqb_words, 1)
        load_w(wb[2], Wqb_words, 2)
        load_w(wb[3], Wqb_words, 3)

        nc.vector.tensor_scalar(out=turns[:, :, 0:1], in0=pos[:].unsqueeze(2), scalar1=1.0 / (2.0 * math.pi), scalar2=None, op0=MUL)
        for j in range(6):
            m = 1 << j
            nc.vector.tensor_scalar(out=turns[:, :, m : 2 * m], in0=turns[:, :, 0:m], scalar1=THETA ** (-m / 64.0), scalar2=None, op0=MUL)
        nc.vector.tensor_scalar(out=kint[:, 0], in0=turns[:], scalar1=0.25, scalar2=None, op0=ADD)
        nc.vector.tensor_scalar(out=kint[:, 1], in0=turns[:], scalar1=0.0, scalar2=None, op0=ADD)
        nc.vector.scalar_tensor_tensor(out=frac[:, 0], in0=turns[:], scalar=0.25, in1=kint[:, 0], op0=ADD, op1=SUB)
        nc.vector.tensor_tensor(out=frac[:, 1], in0=turns[:], in1=kint[:, 1], op=SUB)
        two_pi = 2.0 * math.pi
        for half in range(2):
            c0 = 64 * half
            nc.scalar.activation(out=tab[:, :, 0, c0 : c0 + 64], in_=frac[:, 0], func=ACT.Sin, scale=two_pi)
            nc.scalar.activation(out=tab[:, :, 1, c0 : c0 + 64 : 2], in_=frac[:, 1, :, 1::2], func=ACT.Sin, scale=two_pi)
            nc.scalar.activation(out=tab[:, :, 1, c0 + 1 : c0 + 64 : 2], in_=frac[:, 1, :, 0::2], func=ACT.Sin, scale=-two_pi)

        def cast_s(i, lo, hi):
            nc.scalar.copy(out=xb[i][:, lo:hi], in_=x8[i][:, lo:hi].bitcast(FP8))

        def cast_g(i, lo, hi):
            nc.gpsimd.tensor_copy(out=xb[i][:, lo:hi], in_=x8[i][:, lo:hi].bitcast(FP8))

        sorted_x = set()

        def cast_v(i, lo, hi):
            for c in range(lo, hi, 512):
                nc.vector.tensor_scalar(
                    out=xb[i][:, c : c + 512].rearrange("p (u q e) -> p q u e", u=2, e=2),
                    in0=x8[i][:, c : c + 512].bitcast(FP8).rearrange("p (q u e) -> p q u e", u=2, e=2),
                    scalar1=one32[:],
                    scalar2=None,
                    op0=MUL,
                )
                sorted_x.add((i, c // 512))


        trx = {}

        def turn_x(i, half, b):
            pt = bank(b, [P, 2, 2, P], F32, "trx%d_%d" % (i, half))
            trx[i, half] = pt
            words = xb[i][:].bitcast(F32)
            for g in (2 * half, 2 * half + 1):
                for u in range(2):
                    w0 = 256 * g
                    cols = slice(w0 + P * u, w0 + P * (u + 1)) if (i, g) in sorted_x else slice(w0 + u, w0 + 256, 2)
                    nc.tensor.transpose(pt[:, g - 2 * half, u, :], words[:, cols], ident[:])

        def scale_x(i, g):
            pt = trx[i, g // 2]
            src = pt[:, g % 2].rearrange("p u r -> p (u r)").bitcast(BF16)
            nc.vector.tensor_tensor(
                out=xg[i][:, 512 * g : 512 * (g + 1)].rearrange("p (r u e) -> p r u e", u=2, e=2),
                in0=src.rearrange("p (u r e) -> p r u e", u=2, e=2),
                in1=xs[:, g].rearrange("p (u e) -> p u e", u=2).unsqueeze(1).to_broadcast([P, P, 2, 2]),
                op=MUL,
            )

        planes = {}

        def plane_x(i, g):
            pt = trx[i, g // 2]
            xp = work.tile([P, 4, P], BF16, name="xp", bufs=4)
            planes[i, g] = xp
            for t in range(4):
                u, e = divmod(t, 2)
                nc.scalar.activation(
                    out=xp[:, t, :],
                    in_=pt[:, g % 2, u, :].bitcast(BF16)[:, e::2],
                    func=ACT.Copy,
                    scale=xs[:, g, t : t + 1],
                )

        def spread_x(i, g):
            pt = trx[i, g // 2]
            dst = xg[i][:, 512 * g : 512 * (g + 1)].rearrange("p (r t) -> p r t", t=4)
            for t in range(4):
                u, e = divmod(t, 2)
                nc.scalar.activation(
                    out=dst[:, :, t],
                    in_=pt[:, g % 2, u, :].bitcast(BF16)[:, e::2],
                    func=ACT.Copy,
                    scale=xs[:, g, t : t + 1],
                )

        def weave_x(i, g):
            nc.gpsimd.tensor_scalar(
                out=xg[i][:, 512 * g : 512 * (g + 1)].rearrange("p (r t) -> p r t", t=4),
                in0=planes[i, g][:].rearrange("p t r -> p r t"),
                scalar1=1.0,
                scalar2=0.0,
                op0=MUL,
                op1=ADD,
            )

        def quant_x(i, g0, g1):
            nc.vector.quantize_mx(
                out=xq[i][:, P * g0 : P * g1].bitcast(FP8X4),
                scales=xqs[i][:, P * g0 : P * g1],
                in_=xg[i][:, 512 * g0 : 512 * g1],
            )

        acc = {}

        def mm_a(i, n, b, groups=range(GA)):
            if (i, n) not in acc:
                acc[i, n] = bank(b, [P, 512], F32, "c%d_%d" % (i, n))
            for g in groups:
                nc.tensor.matmul_mx(
                    out=acc[i, n][:],
                    lhsT=xq[i][:, P * g : P * (g + 1)].bitcast(FP8X4),
                    lhsT_scale=xqs[i][:, P * g : P * (g + 1)],
                    rhs=wa[n][:, g].bitcast(FP8X4),
                    rhs_scale=was[4 * g : P, 512 * n : 512 * (n + 1)],
                    start=(g == 0),
                    stop=(g == GA - 1),
                )

        def square(i, n):
            junk = work.tile([P, 512], BF16, name="junk", bufs=2)
            nc.scalar.activation(out=junk[:], in_=acc[i, n][:], func=ACT.Square, accum_out=ssq[i][:, n : n + 1])

        def rms_a(i):
            nc.scalar.activation(out=rms[i][:, 4:7], in_=ssq[i][:, 0:3], func=ACT.Copy, accum_out=rms[i][:, 0:1])

        def rms_b(i):
            nc.gpsimd.tensor_scalar(out=rms[i][:, 2:3], in0=rms[i][:, 0:1], scalar1=1.0 / RQ, scalar2=EPS, op0=MUL, op1=ADD)
            nc.gpsimd.tensor_tensor(out=rms[i][:, 3:4], in0=rms[i][:, 2:3], in1=mhalf[:], op=mybir.AluOpType.pow)

        by_word = "p (q u e) -> p u q e"

        def norm(i, n):
            for u in range(2):
                cols = slice(512 * n + 256 * u, 512 * n + 256 * (u + 1))
                nc.vector.scalar_tensor_tensor(
                    out=hb[i][:, cols].rearrange("p (q e) -> p q e", e=2),
                    in0=acc[i, n][:].rearrange(by_word, u=2, e=2)[:, u],
                    scalar=rms[i][:, 3:4],
                    in1=gbc[:, 512 * n : 512 * (n + 1)].rearrange(by_word, u=2, e=2)[:, u],
                    op0=MUL,
                    op1=MUL,
                )

        hs = {}

        def norm_s(i, n):
            t = work.tile([P, 512], F32, name="hs", bufs=3)
            hs[i, n] = t
            nc.scalar.activation(
                out=t[:].rearrange("p (u q e) -> p u q e", u=2, e=2),
                in_=acc[i, n][:].rearrange(by_word, u=2, e=2),
                func=ACT.Copy,
                scale=rms[i][:, 3:4],
            )

        def norm_g(i, n):
            cols = slice(512 * n, 512 * (n + 1))
            sorted_words = "p (u q e) -> p u q e"
            nc.gpsimd.tensor_tensor(
                out=hb[i][:, cols].rearrange(sorted_words, u=2, e=2),
                in0=hs[i, n][:].rearrange(sorted_words, u=2, e=2),
                in1=gbc[:, cols].rearrange(by_word, u=2, e=2),
                op=MUL,
            )

        trh = {}

        def turn_h(i, part, b):
            words = hb[i][:].bitcast(F32)
            pt = bank(b, [P, 2, 2, P], F32, "trh%d_%d" % (i, part))
            trh[i, part] = pt
            for g in range(2 * part, min(2 * part + 2, GB)):
                for u in range(2):
                    w0 = 256 * g + P * u
                    nc.tensor.transpose(pt[:, g - 2 * part, u, :], words[:, w0 : w0 + P], ident[:])

        def copy_h(i, part, eng=None):
            n = 2 - part
            c0 = 1024 * part
            copy = nc.scalar.copy if eng is None else eng.tensor_copy
            copy(
                out=hg[i][:, c0 : c0 + 512 * n].bitcast(F32).rearrange("p (g r u) -> p g r u", g=n, u=2),
                in_=trh[i, part][:, 0:n].rearrange("p g u r -> p g r u"),
            )

        def quant_h(i, part):
            n = 2 - part
            c0 = 256 * part
            nc.vector.quantize_mx(
                out=hq[i][:, c0 : c0 + P * n].bitcast(FP8X4),
                scales=hqs[i][:, c0 : c0 + P * n],
                in_=hg[i][:, 4 * c0 : 4 * c0 + 512 * n],
            )

        qacc = {}

        def mm_b(i, n, b):
            t = bank(b, [P, WB], F32, "q%d_%d" % (i, n))
            qacc[i, n] = t
            for c0, c1 in ((0, 256), (256, WB)):
                for g in range(GB):
                    nc.tensor.matmul_mx(
                        out=t[:, c0:c1],
                        lhsT=hq[i][:, P * g : P * (g + 1)].bitcast(FP8X4),
                        lhsT_scale=hqs[i][:, P * g : P * (g + 1)],
                        rhs=wb[n // 2][:, g, WB * (n % 2) + c0 : WB * (n % 2) + c1].bitcast(FP8X4),
                        rhs_scale=wbs[4 * g : P, WB * n + c0 : WB * n + c1],
                        start=(g == 0),
                        stop=(g == GB - 1),
                    )

        def nope(i, n):
            b, par = divmod(i, 2)
            nc.scalar.copy(
                out=osb[b][:, 2 * n : 2 * n + 2, par, 0:DN],
                in_=qacc[i, n][:].rearrange("p (h d) -> p h d", h=2)[:, :, 0:DN],
            )

        prod = {}

        def rope_mul(i, n):
            t = work.tile([P, 2, 2, DR], F32, name="prod", bufs=8)
            prod[i, n] = t
            nc.vector.tensor_tensor(
                out=t[:],
                in0=qacc[i, n][:].rearrange("p (h d) -> p h d", h=2)[:, :, DN:DH].unsqueeze(1).to_broadcast([P, 2, 2, DR]),
                in1=tab[:, i % 2].unsqueeze(2).to_broadcast([P, 2, 2, DR]),
                op=MUL,
            )

        turned = {}
        pairs = "p h (i two) -> p h i two"

        def swap(i, n):
            t = work.tile([P, 2, DR], F32, name="turned", bufs=4)
            turned[i, n] = t
            nc.scalar.copy(out=t[:].rearrange(pairs, two=2), in_=prod[i, n][:, 1].rearrange(pairs, two=2)[:, :, :, ::-1])

        def rope_add(i, n, eng):
            b, par = divmod(i, 2)
            t = prod[i, n]
            if (i, n) in turned:
                eng.tensor_tensor(out=osb[b][:, 2 * n : 2 * n + 2, par, DN:DH], in0=t[:, 0], in1=turned[i, n][:], op=ADD)
            else:
                eng.tensor_tensor(
                    out=osb[b][:, 2 * n : 2 * n + 2, par, DN:DH].rearrange(pairs, two=2),
                    in0=t[:, 0].rearrange(pairs, two=2),
                    in1=t[:, 1].rearrange(pairs, two=2)[:, :, :, ::-1],
                    op=ADD,
                )

        def store(b, n):
            nc.sync.dma_start(
                out=out[b].rearrange("h (p two) d -> p h (two d)", two=2)[:, 2 * n : 2 * n + 2, :],
                in_=osb[b][:, 2 * n : 2 * n + 2].rearrange("p h two d -> p h (two d)"),
            )

        def store_one(i, n):
            b, par = divmod(i, 2)
            nc.sync.dma_start(
                out=out[b].rearrange("h (p two) d -> p h two d", two=2)[:, 2 * n : 2 * n + 2, par, :],
                in_=osb[b][:, 2 * n : 2 * n + 2, par, :],
            )

        gain_ps = {}

        def gain_mm(n, b):
            gp = bank(b, [P, 512], BF16, "gain%d" % (n,))
            gain_ps[n] = gp
            nc.tensor.matmul(gp[:], ones[:], gz[:, 512 * n : 512 * (n + 1)], start=True, stop=True)

        def gain_copy(n, copy):
            copy(out=gbc[:, 512 * n : 512 * (n + 1)], in_=gain_ps[n][:])

        warm_ps = bank(7, [P, P], F32, "warm_ps")
        for k in range(24):
            nc.tensor.matmul(warm_ps[:], ones[:], ones[:], start=True, stop=True)
        cast_v(0, 0, 1024)
        gain_mm(1, 0)
        gain_mm(0, 1)
        cast_v(0, 1024, 2048)
        gain_copy(1, nc.scalar.copy)
        turn_x(0, 0, 2)
        gain_copy(0, nc.scalar.copy)
        cast_v(1, 1024, 2048)
        gain_mm(2, 3)
        cast_s(1, 0, 1024)
        turn_x(0, 1, 4)
        scale_x(0, 0)
        turn_x(1, 1, 5)
        scale_x(0, 1)
        plane_x(0, 3)
        turn_x(1, 0, 6)
        quant_x(0, 0, 1)
        spread_x(1, 2)
        quant_x(0, 1, 2)
        scale_x(0, 2)
        weave_x(0, 3)
        mm_a(0, 0, 7, (0,))
        mm_a(0, 0, 0, (1,))
        scale_x(1, 1)
        quant_x(0, 3, 4)
        quant_x(0, 2, 3)
        scale_x(1, 0)
        gain_copy(2, nc.scalar.copy)
        mm_a(0, 0, 0, (2,))
        spread_x(1, 3)
        mm_a(0, 0, 0, (3,))
        mm_a(0, 1, 0)
        quant_x(1, 0, 2)
        cast_v(2, 1024, 2048)
        cast_v(2, 0, 1024)
        square(0, 1)
        turn_x(2, 1, 1)
        quant_x(1, 2, 4)
        square(0, 0)
        turn_x(2, 0, 2)
        scale_x(2, 2)
        mm_a(1, 1, 4)
        plane_x(2, 1)
        scale_x(2, 3)
        cast_v(3, 1024, 2048)
        mm_a(0, 2, 3)
        square(1, 1)
        quant_x(2, 2, 4)
        scale_x(2, 0)
        weave_x(2, 1)
        mm_a(1, 2, 6)
        square(0, 2)
        cast_v(3, 0, 1024)
        rms_a(0)
        mm_a(1, 0, 5)
        quant_x(2, 0, 2)
        square(1, 2)
        rms_b(0)
        norm(0, 1)
        mm_a(2, 0, 1)
        square(1, 0)
        norm(0, 2)
        rms_a(1)
        mm_a(2, 1, 2)
        norm(0, 0)
        rms_b(1)
        square(2, 0)
        norm(1, 0)
        norm_s(1, 2)
        turn_h(0, 1, 0)
        turn_h(0, 0, 3)
        square(2, 1)
        norm(1, 1)
        norm_g(1, 2)
        turn_x(3, 0, 7)
        turn_x(3, 1, 6)
        copy_h(0, 0)
        copy_h(0, 1, nc.vector)
        mm_a(2, 2, 5)
        scale_x(3, 3)
        plane_x(3, 0)
        quant_h(0, 0)
        spread_x(3, 1)
        quant_h(0, 1)
        weave_x(3, 0)
        scale_x(3, 2)
        turn_h(1, 1, 4)
        turn_h(1, 0, 0)
        copy_h(1, 1, nc.vector)
        mm_b(0, 2, 3)
        quant_x(3, 2, 4)
        quant_h(1, 1)
        mm_b(0, 4, 6)
        square(2, 2)
        rope_mul(0, 2)
        mm_b(0, 3, 4)
        copy_h(1, 0)
        quant_x(3, 0, 2)
        rope_mul(0, 4)
        mm_b(0, 7, 7)
        nope(0, 2)
        nope(0, 3)
        quant_h(1, 0)
        rms_a(2)
        nope(0, 4)
        mm_a(3, 2, 0)
        rope_mul(0, 3)
        rope_add(0, 4, nc.gpsimd)
        nope(0, 7)
        rope_mul(0, 7)
        rms_b(2)
        mm_b(1, 4, 3)
        rope_add(0, 3, nc.vector)
        square(3, 2)
        norm(2, 0)
        rope_add(0, 7, nc.gpsimd)
        mm_b(1, 2, 6)
        norm_s(2, 1)
        norm(2, 2)
        mm_b(1, 7, 4)
        nope(1, 4)
        nope(1, 2)
        norm_g(2, 1)
        rope_mul(1, 4)
        mm_b(1, 5, 7)
        nope(1, 7)
        rope_mul(1, 2)
        mm_b(1, 0, 1)
        rope_add(1, 4, nc.gpsimd)
        nope(1, 5)
        rope_mul(1, 7)
        mm_a(3, 1, 2)
        nope(1, 0)
        rope_add(1, 2, nc.gpsimd)
        rope_mul(1, 5)
        store(0, 4)
        rope_add(1, 7, nc.vector)
        mm_a(3, 0, 5)
        rope_mul(1, 0)
        rope_add(1, 5, nc.gpsimd)
        square(3, 1)
        store(0, 7)
        rope_add(0, 2, nc.vector)
        mm_b(1, 6, 3)
        rope_add(1, 0, nc.gpsimd)
        square(3, 0)
        store(0, 2)
        mm_b(1, 3, 6)
        rope_mul(1, 6)
        rms_a(3)
        mm_b(1, 1, 4)
        rms_b(3)
        rope_mul(1, 3)
        nope(1, 6)
        rope_add(1, 6, nc.gpsimd)
        mm_b(0, 5, 7)
        norm_s(3, 1)
        norm(3, 0)
        rope_add(1, 3, nc.gpsimd)
        nope(1, 1)
        mm_b(0, 1, 1)
        nope(1, 3)
        norm(3, 2)
        nope(0, 5)
        norm_g(3, 1)
        store(0, 3)
        turn_h(2, 0, 3)
        rope_mul(1, 1)
        nope(0, 1)
        turn_h(3, 1, 2)
        turn_h(2, 1, 5)
        copy_h(2, 0)
        rope_mul(0, 5)
        mm_b(0, 0, 6)
        rope_add(1, 1, nc.gpsimd)
        copy_h(3, 1)
        rope_mul(0, 1)
        copy_h(2, 1)
        turn_h(3, 0, 0)
        nope(0, 0)
        quant_h(2, 0)
        mm_b(0, 6, 4)
        copy_h(3, 0)
        quant_h(2, 1)
        rope_add(0, 5, nc.vector)
        quant_h(3, 1)
        mm_b(2, 1, 3)
        rope_mul(0, 0)
        rope_add(0, 1, nc.gpsimd)
        store(0, 5)
        nope(0, 6)
        mm_b(2, 2, 7)
        quant_h(3, 0)
        nope(2, 1)
        store(0, 1)
        rope_add(0, 0, nc.gpsimd)
        rope_mul(0, 6)
        mm_b(2, 6, 2)
        nope(2, 2)
        rope_mul(2, 1)
        rope_add(0, 6, nc.gpsimd)
        mm_b(3, 6, 5)
        store(0, 0)
        nope(2, 6)
        rope_mul(2, 2)
        rope_add(2, 1, nc.gpsimd)
        mm_b(3, 3, 1)
        store(0, 6)
        nope(3, 6)
        rope_mul(2, 6)
        mm_b(3, 1, 0)
        rope_add(2, 2, nc.gpsimd)
        rope_mul(3, 6)
        nope(3, 3)
        mm_b(2, 3, 6)
        rope_add(2, 6, nc.gpsimd)
        rope_mul(3, 3)
        nope(3, 1)
        mm_b(2, 4, 4)
        rope_add(3, 6, nc.gpsimd)
        rope_mul(3, 1)
        nope(2, 3)
        mm_b(3, 2, 3)
        rope_mul(2, 3)
        rope_add(3, 1, nc.gpsimd)
        nope(2, 4)
        store(1, 6)
        rope_mul(2, 4)
        mm_b(3, 4, 7)
        nope(3, 2)
        rope_add(2, 3, nc.gpsimd)
        store(1, 1)
        rope_mul(3, 2)
        mm_b(2, 5, 2)
        nope(3, 4)
        rope_add(3, 3, nc.vector)
        mm_b(3, 5, 5)
        rope_add(2, 4, nc.vector)
        nope(2, 5)
        store(1, 3)
        rope_add(3, 2, nc.gpsimd)
        rope_mul(3, 4)
        mm_b(2, 0, 1)
        nope(3, 5)
        rope_mul(2, 5)
        rope_add(3, 4, nc.gpsimd)
        mm_b(3, 0, 0)
        store(1, 2)
        nope(2, 0)
        rope_mul(3, 5)
        mm_b(3, 7, 6)
        rope_add(2, 5, nc.gpsimd)
        store(1, 4)
        nope(3, 0)
        rope_mul(2, 0)
        mm_b(2, 7, 4)
        rope_add(3, 5, nc.gpsimd)
        nope(3, 7)
        rope_mul(3, 0)
        rope_add(2, 0, nc.gpsimd)
        rope_mul(3, 7)
        nope(2, 7)
        store(1, 5)
        rope_add(3, 0, nc.vector)
        rope_mul(2, 7)
        rope_add(3, 7, nc.gpsimd)
        store(1, 0)
        rope_add(2, 7, nc.vector)
        store_one(3, 7)
        store_one(2, 7)
